import numpy as np
import ml_dtypes


def mxq(x, axis, fmt="e4m3"):
    dtype, down = {"e4m3": (ml_dtypes.float8_e4m3fn, 7), "e5m2": (ml_dtypes.float8_e5m2, 14)}[fmt]
    v = np.moveaxis(np.asarray(x, np.float32).astype(ml_dtypes.bfloat16).astype(np.float64), axis, -1)
    blocks = v.reshape(v.shape[:-1] + (-1, 32))
    amax = np.abs(blocks).max(-1, keepdims=True)
    byte = np.maximum(np.where(amax > 0, np.frexp(amax)[1] - 1 + 127, 0) - down, 1)
    scale = np.exp2(byte - 127.0)
    codes = (blocks / scale).astype(np.float32).astype(dtype).astype(np.float64)
    return np.moveaxis((codes * scale).reshape(v.shape), -1, axis)


WIDE = False


def mx_kscale(k):
    if not WIDE:
        return np.ones(k)
    levels = np.array([10, -10, 5, -5, 0])
    a = np.random.permutation(np.resize(levels, k // 512 * 4)).reshape(k // 512, 4)
    idx = np.arange(k)
    return np.exp2(a[idx // 512, idx % 128 // 32])


BF16 = ml_dtypes.bfloat16


def bf(x):
    return np.asarray(x, np.float32).astype(BF16)


def f64(x):
    return np.asarray(x).astype(np.float64)


B, I, O, G = 128, 128, 1024, 5
DEGREE = 3
NB = G + DEGREE
GRID_MIN, GRID_MAX = -1.0, 1.0
EPS = 1e-8
BLK = 32


def extended_grid():
    h = (GRID_MAX - GRID_MIN) / G
    return GRID_MIN + h * f64(np.arange(-DEGREE, G + DEGREE + 1))


def bspline_basis(x):
    t = extended_grid()
    G0 = G + 2 * DEGREE
    xe = x[..., None]
    basis = ((xe >= t[:-1]) & (xe < t[1:])).astype(np.float64)
    for k in range(1, DEGREE + 1):
        cnt = G0 - k
        left_den = t[k:k + cnt] - t[:cnt]
        right_den = t[k + 1:k + 1 + cnt] - t[1:1 + cnt]
        left_term = np.where(left_den > EPS, (xe - t[:cnt]) / np.where(left_den > EPS, left_den, 1.0), 0.0)
        right_term = np.where(right_den > EPS, (t[k + 1:k + 1 + cnt] - xe) / np.where(right_den > EPS, right_den, 1.0), 0.0)
        basis = left_term * basis[..., :-1] + right_term * basis[..., 1:]
    return basis


def setup_inputs():
    s = mx_kscale(I * NB)
    e = np.repeat(s[::BLK], BLK)
    hot = (e > np.sqrt(e.max() * e.min())).reshape(I, NB)
    huge = e.max() / e.min()
    park = hot.any(axis=1)
    x = np.random.standard_normal((B, I))
    x = np.where(park[None, :], 1.0 + np.abs(x), x)
    dead = (np.arange(NB) < G)[None, :]
    f = np.where(hot & dead, huge, np.where(hot, 0.0, 1.0))
    return {"x": bf(x),
            "spline_coeffs": bf(np.random.standard_normal((O, I, NB)) * 2.0 / np.sqrt(I) * f[None]),
            "residual_weight": bf(np.random.standard_normal((O, I)) / np.sqrt(I)),
            "residual_bias": bf(np.random.standard_normal(O) * 0.3),
            "scale_base": bf(np.random.uniform(0.5, 1.5, (O, 1)) + 0.3 * np.random.standard_normal((O, I)))}


def reference(x, spline_coeffs, residual_weight, residual_bias, scale_base):
    x = f64(x)
    x_clamped = np.clip(x, GRID_MIN, GRID_MAX)
    basis = bspline_basis(x_clamped)
    spline_out = mxq(basis.reshape(B, I * NB), 1, "e4m3") @ mxq(f64(spline_coeffs).reshape(O, I * NB), 1, "e4m3").T
    residual_out = x @ f64(residual_weight).T + f64(residual_bias)
    scale = np.mean(f64(scale_base), axis=1)
    return spline_out * scale + residual_out

@@ -1,0 +1,227 @@
+from contextlib import ExitStack
+import math
+
+import concourse.mybir as mybir
+from concourse.masks import make_identity
+
+F32 = mybir.dt.float32
+BF16 = mybir.dt.bfloat16
+I32 = mybir.dt.int32
+U32 = mybir.dt.uint32
+U8 = mybir.dt.uint8
+FP8X4 = mybir.dt.float8_e4m3fn_x4
+ALU = mybir.AluOpType
+ACT = mybir.ActivationFunctionType
+AX = mybir.AxisListType
+
+P = 128
+NB = 8
+K = P * NB
+O = 1024
+O_TILES = O // P
+PASSES = 2
+PER_BANK = 4
+
+FLOPS = 2 * P * K * O + 2 * P * P * O
+
+
+def tile_bsplinebasis_v2_s_kernel(
+    tc, x, spline_coeffs, residual_weight, residual_bias, scale_base, out
+):
+    nc = tc.nc
+    with ExitStack() as ctx:
+        const = ctx.enter_context(tc.tile_pool(name="const", bufs=1))
+        keep = ctx.enter_context(tc.tile_pool(name="keep", bufs=1))
+        work = ctx.enter_context(tc.tile_pool(name="work", bufs=2))
+        coef_pool = ctx.enter_context(tc.tile_pool(name="coef", bufs=O_TILES))
+        stage = ctx.enter_context(tc.tile_pool(name="stage", bufs=3))
+        psum_t = ctx.enter_context(tc.psum_pool(name="psum_t", bufs=4))
+        psum_io = ctx.enter_context(tc.psum_pool(name="psum_io", bufs=2))
+        psum_mx = ctx.enter_context(tc.psum_pool(name="psum_mx", bufs=2))
+
+        x_sb = keep.tile([P, P], BF16)
+        nc.sync.dma_start(out=x_sb[:], in_=x)
+        coef_sb = []
+        for c in range(O_TILES):
+            coef_c = coef_pool.tile([P, K], BF16, name="coef_c")
+            nc.sync.dma_start(
+                out=coef_c[:],
+                in_=spline_coeffs[c * P : (c + 1) * P].rearrange("o i j -> o (i j)"),
+            )
+            coef_sb.append(coef_c)
+        bias_rows = keep.tile([P, P], BF16)
+        nc.vector.memset(bias_rows[:], 0.0)
+        nc.scalar.dma_start(
+            out=bias_rows[0:O_TILES, :], in_=residual_bias.rearrange("(c p) -> c p", p=P)
+        )
+        base_sb = keep.tile([P, O_TILES, P], BF16)
+        nc.scalar.dma_start(out=base_sb[:], in_=scale_base.rearrange("(c p) i -> p c i", p=P))
+        rw_sb = keep.tile([P, O_TILES, P], BF16)
+        nc.scalar.dma_start(
+            out=rw_sb[:], in_=residual_weight.rearrange("(c p) i -> p c i", p=P)
+        )
+
+        ident_f32 = const.tile([P, P], F32)
+        make_identity(nc, ident_f32[:])
+        ident_bf = const.tile([P, P], BF16)
+        nc.vector.tensor_copy(out=ident_bf[:], in_=ident_f32[:])
+        part_index = const.tile([P, 1], I32)
+        nc.gpsimd.iota(part_index[:], pattern=[[0, 1]], base=0, channel_multiplier=1)
+        part_mod4 = const.tile([P, 1], I32)
+        nc.vector.tensor_single_scalar(
+            out=part_mod4[:], in_=part_index[:], scalar=3, op=ALU.bitwise_and
+        )
+        part_mod4_f = const.tile([P, 1], F32)
+        nc.vector.tensor_copy(out=part_mod4_f[:], in_=part_mod4[:])
+        centre = const.tile([P, 2], F32)
+        for e in range(2):
+            nc.vector.tensor_scalar(
+                out=centre[:, e : e + 1],
+                in0=part_mod4_f[:],
+                scalar1=-2.0,
+                scalar2=3.5 - e,
+                op0=ALU.mult,
+                op1=ALU.add,
+            )
+        zero_col = const.tile([P, 1], F32)
+        nc.vector.memset(zero_col[:], 0.0)
+        warm = const.tile([P, 1], F32)
+        nc.scalar.activation(out=warm[:], in_=zero_col[:], func=ACT.Abs)
+
+        clamped = keep.tile([P, P, 4], BF16)
+        nc.vector.tensor_scalar(
+            out=clamped[:],
+            in0=x_sb[:].unsqueeze(2).to_broadcast([P, P, 4]),
+            scalar1=-1.0,
+            scalar2=1.0,
+            op0=ALU.max,
+            op1=ALU.min,
+        )
+        u_ps = psum_io.tile([P, 4, P], BF16, tag="io")
+        clamped_cols = clamped[:].rearrange("b i r -> b (i r)")
+        for m in range(4):
+            nc.tensor.transpose(u_ps[:, m, :], clamped_cols[:, m * P : (m + 1) * P], ident_bf[:])
+        small_ps = psum_mx.tile([P, 2, P], BF16, tag="mx")
+        nc.tensor.transpose(small_ps[:, 0, :], x_sb[:], ident_bf[:])
+        xT_sb = keep.tile([P, P], BF16)
+        nc.vector.tensor_copy(out=xT_sb[:], in_=small_ps[:, 0, :])
+
+        basis_codes = keep.tile([P, PASSES, P], U32, align_bytes=64)
+        basis_scales = keep.tile([P, PASSES, P], U8, align_bytes=64)
+        root_sixth = 1.0 / math.sqrt(6.0)
+        root_two_thirds = math.sqrt(2.0 / 3.0)
+        for g in range(PASSES):
+            dist = work.tile([P, 2, 2 * P], F32)
+            for e in range(2):
+                nc.scalar.activation(
+                    out=dist[:, e, :].rearrange("p (b u) -> p b u", u=2),
+                    in_=u_ps[:, 2 * g : 2 * g + 2, :].rearrange("p u b -> p b u"),
+                    func=ACT.Abs,
+                    scale=2.5,
+                    bias=centre[:, e : e + 1],
+                )
+            wide_sq = work.tile([P, 2, 2 * P], F32)
+            nc.scalar.activation(
+                out=wide_sq[:], in_=dist[:], func=ACT.Square,
+                scale=root_sixth, bias=-2.0 * root_sixth,
+            )
+            narrow_sq = work.tile([P, 2, 2 * P], F32)
+            nc.scalar.activation(
+                out=narrow_sq[:], in_=dist[:], func=ACT.Square,
+                scale=root_two_thirds, bias=-root_two_thirds,
+            )
+            wide_cube = work.tile([P, 2, 2 * P], F32)
+            nc.vector.scalar_tensor_tensor(
+                out=wide_cube[:], in0=dist[:], scalar=2.0, in1=wide_sq[:],
+                op0=ALU.subtract, op1=ALU.mult,
+            )
+            narrow_cube = work.tile([P, 2, 2 * P], F32)
+            nc.vector.scalar_tensor_tensor(
+                out=narrow_cube[:], in0=dist[:], scalar=1.0, in1=narrow_sq[:],
+                op0=ALU.subtract, op1=ALU.mult,
+            )
+            wide_cut = work.tile([P, 2, 2 * P], F32)
+            nc.vector.tensor_scalar_min(out=wide_cut[:], in0=wide_cube[:], scalar1=0.0)
+            basis_bf = work.tile([P, 2 * P, 2], BF16, align_bytes=64)
+            nc.vector.scalar_tensor_tensor(
+                out=basis_bf[:],
+                in0=narrow_cube[:].rearrange("p e n -> p n e"),
+                scalar=0.0,
+                in1=wide_cut[:].rearrange("p e n -> p n e"),
+                op0=ALU.min,
+                op1=ALU.subtract,
+            )
+            nc.vector.quantize_mx(
+                out=basis_codes[:, g, :].bitcast(FP8X4),
+                scales=basis_scales[:, g, :],
+                in_=basis_bf[:].rearrange("p n e -> p (n e)"),
+            )
+
+        rwT_ps = psum_io.tile([P, O_TILES, P], BF16, tag="io")
+        for c in range(O_TILES):
+            nc.tensor.transpose(rwT_ps[:, c, :], rw_sb[:, c, :], ident_bf[:])
+        rwT_sb = keep.tile([P, O_TILES, P], BF16)
+        nc.vector.tensor_copy(out=rwT_sb[:], in_=rwT_ps[:])
+
+        nc.tensor.transpose(small_ps[:, 1, :], bias_rows[:], ident_bf[:])
+        bias_col = keep.tile([P, O_TILES], F32)
+        nc.vector.tensor_copy(out=bias_col[:], in_=small_ps[:, 1, 0:O_TILES])
+
+        base_sum = keep.tile([P, O_TILES], F32)
+        nc.vector.tensor_reduce(out=base_sum[:], in_=base_sb[:], axis=AX.X, op=ALU.add)
+        scale_col = keep.tile([P, O_TILES], F32)
+        nc.vector.tensor_scalar_mul(out=scale_col[:], in0=base_sum[:], scalar1=1.0 / P)
+
+        coef_codes = keep.tile([P, O_TILES, PASSES * P], U32, align_bytes=64)
+        coef_scales = keep.tile([P, O_TILES, PASSES * P], U8, align_bytes=64)
+        spline_ps = None
+        out_ps = None
+        for c in range(O_TILES):
+            slot = c % PER_BANK
+            if slot == 0:
+                spline_ps = psum_mx.tile([P, PER_BANK, P], F32, tag="mx")
+                out_ps = psum_io.tile([P, PER_BANK, P], F32, tag="io")
+
+            coef_words = coef_sb[c][:].bitcast(F32)
+            words_ps = psum_t.tile([P, 2 * PASSES, P], F32)
+            for m in range(2 * PASSES):
+                nc.tensor.transpose(
+                    words_ps[:, m, :], coef_words[:, m * P : (m + 1) * P], ident_f32[:]
+                )
+            grouped = stage.tile([P, PASSES, P, 4], BF16, align_bytes=64)
+            nc.scalar.copy(
+                out=grouped[:].bitcast(F32),
+                in_=words_ps[:].rearrange("p (g u) o -> p g o u", u=2),
+            )
+            nc.vector.quantize_mx(
+                out=coef_codes[:, c, :].bitcast(FP8X4),
+                scales=coef_scales[:, c, :],
+                in_=grouped[:].rearrange("p g o t -> p (g o t)"),
+            )
+            for g in range(PASSES):
+                cols = slice(g * P, (g + 1) * P)
+                nc.tensor.matmul_mx(
+                    out=spline_ps[:, slot, :],
+                    lhsT=coef_codes[:, c, cols].bitcast(FP8X4),
+                    lhsT_scale=coef_scales[:, c, cols],
+                    rhs=basis_codes[:, g, :].bitcast(FP8X4),
+                    rhs_scale=basis_scales[:, g, :],
+                    start=(g == 0),
+                    stop=(g == PASSES - 1),
+                )
+            scaled = stage.tile([P, P], F32)
+            nc.scalar.activation(
+                out=scaled[:], in_=spline_ps[:, slot, :], func=ACT.Identity,
+                scale=scale_col[:, c : c + 1], bias=bias_col[:, c : c + 1],
+            )
+            nc.tensor.matmul(
+                out=out_ps[:, slot, :], lhsT=xT_sb[:], rhs=rwT_sb[:, c, :],
+                start=True, stop=False,
+            )
+            nc.tensor.matmul(
+                out=out_ps[:, slot, :], lhsT=scaled[:], rhs=ident_f32[:],
+                is_transpose=True, start=False, stop=True,
+            )
+            out_sb = stage.tile([P, P], F32)
+            nc.vector.tensor_copy(out=out_sb[:], in_=out_ps[:, slot, :])
+            nc.sync.dma_start(out=out[:, c * P : (c + 1) * P], in_=out_sb[:])

@@ -19,6 +19,7 @@ NB = 8
 K = P * NB
 O = 1024
 O_TILES = O // P
+O_PAIRS = O_TILES // 2
 PASSES = 2
 PER_BANK = 4
 
@@ -30,37 +31,49 @@ def tile_bsplinebasis_v2_s_kernel(
 ):
     nc = tc.nc
     with ExitStack() as ctx:
+        ctx.enter_context(tc.manual_schedule())
         const = ctx.enter_context(tc.tile_pool(name="const", bufs=1))
         keep = ctx.enter_context(tc.tile_pool(name="keep", bufs=1))
         work = ctx.enter_context(tc.tile_pool(name="work", bufs=2))
-        coef_pool = ctx.enter_context(tc.tile_pool(name="coef", bufs=O_TILES))
-        stage = ctx.enter_context(tc.tile_pool(name="stage", bufs=3))
+        coef_pool = ctx.enter_context(tc.tile_pool(name="coef", bufs=O_PAIRS))
+        group_pool = ctx.enter_context(tc.tile_pool(name="group", bufs=O_TILES))
+        stage = ctx.enter_context(tc.tile_pool(name="stage", bufs=4))
         psum_t = ctx.enter_context(tc.psum_pool(name="psum_t", bufs=4))
-        psum_io = ctx.enter_context(tc.psum_pool(name="psum_io", bufs=2))
+        psum_u = ctx.enter_context(tc.psum_pool(name="psum_u", bufs=2))
         psum_mx = ctx.enter_context(tc.psum_pool(name="psum_mx", bufs=2))
 
         x_sb = keep.tile([P, P], BF16)
         nc.sync.dma_start(out=x_sb[:], in_=x)
-        coef_sb = []
-        for c in range(O_TILES):
-            coef_c = coef_pool.tile([P, K], BF16, name="coef_c")
-            nc.sync.dma_start(
-                out=coef_c[:],
-                in_=spline_coeffs[c * P : (c + 1) * P].rearrange("o i j -> o (i j)"),
-            )
-            coef_sb.append(coef_c)
-        bias_rows = keep.tile([P, P], BF16)
-        nc.vector.memset(bias_rows[:], 0.0)
-        nc.scalar.dma_start(
-            out=bias_rows[0:O_TILES, :], in_=residual_bias.rearrange("(c p) -> c p", p=P)
-        )
         base_sb = keep.tile([P, O_TILES, P], BF16)
-        nc.scalar.dma_start(out=base_sb[:], in_=scale_base.rearrange("(c p) i -> p c i", p=P))
-        rw_sb = keep.tile([P, O_TILES, P], BF16)
-        nc.scalar.dma_start(
-            out=rw_sb[:], in_=residual_weight.rearrange("(c p) i -> p c i", p=P)
+        nc.sync.dma_start(
+            out=base_sb[:].rearrange("p (h t) i -> p h (t i)", t=2),
+            in_=scale_base.rearrange("(h p t) i -> p h (t i)", p=P, t=2),
         )
+        rw_sb = keep.tile([P, O_TILES, P], BF16)
+        nc.sync.dma_start(
+            out=rw_sb[:].rearrange("p (h t) i -> p h (t i)", t=2),
+            in_=residual_weight.rearrange("(h p t) i -> p h (t i)", p=P, t=2),
+        )
+        bias_rows = keep.tile([P, 2 * P], BF16)
+        nc.vector.memset(bias_rows[:], 0.0)
+        nc.sync.dma_start(
+            out=bias_rows[0:O_PAIRS, :], in_=residual_bias.rearrange("(h n) -> h n", h=O_PAIRS)
+        )
+        coef_sb = []
+        for h in range(O_PAIRS):
+            coef_h = coef_pool.tile([P, 2, K], BF16, name="coef_h")
+            nc.sync.dma_start(
+                out=coef_h[:],
+                in_=spline_coeffs[2 * h * P : 2 * (h + 1) * P].rearrange(
+                    "(p t) i j -> p t (i j)", t=2
+                ),
+            )
+            coef_sb.append(coef_h)
 
+        zero_col = const.tile([P, 1], F32)
+        nc.vector.memset(zero_col[:], 0.0)
+        warm = const.tile([P, 1], F32)
+        nc.scalar.activation(out=warm[:], in_=zero_col[:], func=ACT.Abs)
         ident_f32 = const.tile([P, P], F32)
         make_identity(nc, ident_f32[:])
         ident_bf = const.tile([P, P], BF16)
@@ -83,28 +96,47 @@ def tile_bsplinebasis_v2_s_kernel(
                 op0=ALU.mult,
                 op1=ALU.add,
             )
-        zero_col = const.tile([P, 1], F32)
-        nc.vector.memset(zero_col[:], 0.0)
-        warm = const.tile([P, 1], F32)
-        nc.scalar.activation(out=warm[:], in_=zero_col[:], func=ACT.Abs)
 
+        half = P // PASSES
         clamped = keep.tile([P, P, 4], BF16)
-        nc.vector.tensor_scalar(
-            out=clamped[:],
-            in0=x_sb[:].unsqueeze(2).to_broadcast([P, P, 4]),
-            scalar1=-1.0,
-            scalar2=1.0,
-            op0=ALU.max,
-            op1=ALU.min,
-        )
-        u_ps = psum_io.tile([P, 4, P], BF16, tag="io")
-        clamped_cols = clamped[:].rearrange("b i r -> b (i r)")
-        for m in range(4):
-            nc.tensor.transpose(u_ps[:, m, :], clamped_cols[:, m * P : (m + 1) * P], ident_bf[:])
-        small_ps = psum_mx.tile([P, 2, P], BF16, tag="mx")
-        nc.tensor.transpose(small_ps[:, 0, :], x_sb[:], ident_bf[:])
+        u_ps = []
+        for g in range(PASSES):
+            feats = slice(g * half, (g + 1) * half)
+            nc.vector.tensor_scalar(
+                out=clamped[:, feats, :],
+                in0=x_sb[:, feats].unsqueeze(2).to_broadcast([P, half, 4]),
+                scalar1=-1.0,
+                scalar2=1.0,
+                op0=ALU.max,
+                op1=ALU.min,
+            )
+            u_g = psum_u.tile([P, 2, P], BF16, name="u_g")
+            for u in range(2):
+                first = g * half + u * (half // 2)
+                nc.tensor.transpose(
+                    u_g[:, u, :],
+                    clamped[:, first : first + half // 2, :].rearrange("b i r -> b (i r)"),
+                    ident_bf[:],
+                )
+            u_ps.append(u_g)
+
+        xT_ps = psum_mx.tile([P, P], BF16, tag="mx")
+        nc.tensor.transpose(xT_ps[:], x_sb[:], ident_bf[:])
         xT_sb = keep.tile([P, P], BF16)
-        nc.vector.tensor_copy(out=xT_sb[:], in_=small_ps[:, 0, :])
+        nc.vector.tensor_copy(out=xT_sb[:], in_=xT_ps[:])
+
+        base_sum = keep.tile([P, O_TILES], F32)
+        nc.vector.tensor_reduce(out=base_sum[:], in_=base_sb[:], axis=AX.X, op=ALU.add)
+        scale_col = keep.tile([P, O_TILES], F32)
+        nc.vector.tensor_scalar_mul(out=scale_col[:], in0=base_sum[:], scalar1=1.0 / P)
+
+        rwT_ps = psum_t.tile([P, O_TILES, P], BF16, tag="t")
+        for c in range(O_TILES):
+            nc.tensor.transpose(rwT_ps[:, c, :], rw_sb[:, c, :], ident_bf[:])
+        bias_ps = psum_mx.tile([P, P], F32, tag="mx")
+        nc.tensor.transpose(bias_ps[:], bias_rows[:].bitcast(F32), ident_f32[:])
+        rwT_sb = keep.tile([P, O_TILES, P], BF16)
+        bias_col = keep.tile([P, O_TILES], F32)
 
         basis_codes = keep.tile([P, PASSES, P], U32, align_bytes=64)
         basis_scales = keep.tile([P, PASSES, P], U8, align_bytes=64)
@@ -115,7 +147,7 @@ def tile_bsplinebasis_v2_s_kernel(
             for e in range(2):
                 nc.scalar.activation(
                     out=dist[:, e, :].rearrange("p (b u) -> p b u", u=2),
-                    in_=u_ps[:, 2 * g : 2 * g + 2, :].rearrange("p u b -> p b u"),
+                    in_=u_ps[g][:].rearrange("p u b -> p b u"),
                     func=ACT.Abs,
                     scale=2.5,
                     bias=centre[:, e : e + 1],
@@ -151,44 +183,27 @@ def tile_bsplinebasis_v2_s_kernel(
                 op0=ALU.min,
                 op1=ALU.subtract,
             )
+            if g == 0:
+                nc.vector.tensor_copy(out=rwT_sb[:], in_=rwT_ps[:])
+                nc.vector.tensor_copy(
+                    out=bias_col[:], in_=bias_ps[:, 0:O_PAIRS].bitcast(BF16)
+                )
             nc.vector.quantize_mx(
                 out=basis_codes[:, g, :].bitcast(FP8X4),
                 scales=basis_scales[:, g, :],
                 in_=basis_bf[:].rearrange("p n e -> p (n e)"),
             )
 
-        rwT_ps = psum_io.tile([P, O_TILES, P], BF16, tag="io")
-        for c in range(O_TILES):
-            nc.tensor.transpose(rwT_ps[:, c, :], rw_sb[:, c, :], ident_bf[:])
-        rwT_sb = keep.tile([P, O_TILES, P], BF16)
-        nc.vector.tensor_copy(out=rwT_sb[:], in_=rwT_ps[:])
-
-        nc.tensor.transpose(small_ps[:, 1, :], bias_rows[:], ident_bf[:])
-        bias_col = keep.tile([P, O_TILES], F32)
-        nc.vector.tensor_copy(out=bias_col[:], in_=small_ps[:, 1, 0:O_TILES])
-
-        base_sum = keep.tile([P, O_TILES], F32)
-        nc.vector.tensor_reduce(out=base_sum[:], in_=base_sb[:], axis=AX.X, op=ALU.add)
-        scale_col = keep.tile([P, O_TILES], F32)
-        nc.vector.tensor_scalar_mul(out=scale_col[:], in0=base_sum[:], scalar1=1.0 / P)
-
         coef_codes = keep.tile([P, O_TILES, PASSES * P], U32, align_bytes=64)
         coef_scales = keep.tile([P, O_TILES, PASSES * P], U8, align_bytes=64)
-        spline_ps = None
-        out_ps = None
         for c in range(O_TILES):
-            slot = c % PER_BANK
-            if slot == 0:
-                spline_ps = psum_mx.tile([P, PER_BANK, P], F32, tag="mx")
-                out_ps = psum_io.tile([P, PER_BANK, P], F32, tag="io")
-
-            coef_words = coef_sb[c][:].bitcast(F32)
-            words_ps = psum_t.tile([P, 2 * PASSES, P], F32)
+            coef_words = coef_sb[c // 2][:, c % 2, :].bitcast(F32)
+            words_ps = psum_t.tile([P, 2 * PASSES, P], F32, tag="t")
             for m in range(2 * PASSES):
                 nc.tensor.transpose(
                     words_ps[:, m, :], coef_words[:, m * P : (m + 1) * P], ident_f32[:]
                 )
-            grouped = stage.tile([P, PASSES, P, 4], BF16, align_bytes=64)
+            grouped = group_pool.tile([P, PASSES, P, 4], BF16, align_bytes=64)
             nc.scalar.copy(
                 out=grouped[:].bitcast(F32),
                 in_=words_ps[:].rearrange("p (g u) o -> p g o u", u=2),
@@ -198,10 +213,16 @@ def tile_bsplinebasis_v2_s_kernel(
                 scales=coef_scales[:, c, :],
                 in_=grouped[:].rearrange("p g o t -> p (g o t)"),
             )
+
+        spline_ps = []
+        for c in range(O_TILES):
+            if c % PER_BANK == 0:
+                spline_bank = psum_mx.tile([P, PER_BANK, P], F32, tag="mx")
+                spline_ps.append(spline_bank)
             for g in range(PASSES):
                 cols = slice(g * P, (g + 1) * P)
                 nc.tensor.matmul_mx(
-                    out=spline_ps[:, slot, :],
+                    out=spline_ps[c // PER_BANK][:, c % PER_BANK, :],
                     lhsT=coef_codes[:, c, cols].bitcast(FP8X4),
                     lhsT_scale=coef_scales[:, c, cols],
                     rhs=basis_codes[:, g, :].bitcast(FP8X4),
@@ -209,19 +230,28 @@ def tile_bsplinebasis_v2_s_kernel(
                     start=(g == 0),
                     stop=(g == PASSES - 1),
                 )
-            scaled = stage.tile([P, P], F32)
-            nc.scalar.activation(
-                out=scaled[:], in_=spline_ps[:, slot, :], func=ACT.Identity,
-                scale=scale_col[:, c : c + 1], bias=bias_col[:, c : c + 1],
+
+        for h in range(O_PAIRS):
+            out_ps = psum_t.tile([P, 2, P], F32, tag="t")
+            for t in range(2):
+                c = 2 * h + t
+                scaled = stage.tile([P, P], F32)
+                nc.scalar.activation(
+                    out=scaled[:], in_=spline_ps[c // PER_BANK][:, c % PER_BANK, :],
+                    func=ACT.Identity,
+                    scale=scale_col[:, c : c + 1], bias=bias_col[:, c : c + 1],
+                )
+                nc.tensor.matmul(
+                    out=out_ps[:, t, :], lhsT=xT_sb[:], rhs=rwT_sb[:, c, :],
+                    start=True, stop=False,
+                )
+                nc.tensor.matmul(
+                    out=out_ps[:, t, :], lhsT=scaled[:], rhs=ident_f32[:],
+                    is_transpose=True, start=False, stop=True,
+                )
+            out_sb = stage.tile([P, P, 2], F32)
+            nc.vector.tensor_copy(out=out_sb[:], in_=out_ps[:].rearrange("b t p -> b p t"))
+            nc.sync.dma_start(
+                out=out[:, 2 * h * P : 2 * (h + 1) * P],
+                in_=out_sb[:].rearrange("b p t -> b (p t)"),
             )
-            nc.tensor.matmul(
-                out=out_ps[:, slot, :], lhsT=xT_sb[:], rhs=rwT_sb[:, c, :],
-                start=True, stop=False,
-            )
-            nc.tensor.matmul(
-                out=out_ps[:, slot, :], lhsT=scaled[:], rhs=ident_f32[:],
-                is_transpose=True, start=False, stop=True,
-            )
-            out_sb = stage.tile([P, P], F32)
-            nc.vector.tensor_copy(out=out_sb[:], in_=out_ps[:, slot, :])
-            nc.sync.dma_start(out=out[:, c * P : (c + 1) * P], in_=out_sb[:])

@@ -37,10 +37,9 @@ def tile_bsplinebasis_v2_s_kernel(
         work = ctx.enter_context(tc.tile_pool(name="work", bufs=2))
         coef_pool = ctx.enter_context(tc.tile_pool(name="coef", bufs=O_PAIRS))
         group_pool = ctx.enter_context(tc.tile_pool(name="group", bufs=O_TILES))
-        stage = ctx.enter_context(tc.tile_pool(name="stage", bufs=4))
+        stage = ctx.enter_context(tc.tile_pool(name="stage", bufs=O_TILES))
         psum_t = ctx.enter_context(tc.psum_pool(name="psum_t", bufs=4))
-        psum_u = ctx.enter_context(tc.psum_pool(name="psum_u", bufs=2))
-        psum_mx = ctx.enter_context(tc.psum_pool(name="psum_mx", bufs=2))
+        psum_s = ctx.enter_context(tc.psum_pool(name="psum_s", bufs=4))
 
         x_sb = keep.tile([P, P], BF16)
         nc.sync.dma_start(out=x_sb[:], in_=x)
@@ -50,15 +49,8 @@ def tile_bsplinebasis_v2_s_kernel(
             in_=scale_base.rearrange("(h p t) i -> p h (t i)", p=P, t=2),
         )
         rw_sb = keep.tile([P, O_TILES, P], BF16)
-        nc.sync.dma_start(
-            out=rw_sb[:].rearrange("p (h t) i -> p h (t i)", t=2),
-            in_=residual_weight.rearrange("(h p t) i -> p h (t i)", p=P, t=2),
-        )
         bias_rows = keep.tile([P, 2 * P], BF16)
         nc.vector.memset(bias_rows[:], 0.0)
-        nc.sync.dma_start(
-            out=bias_rows[0:O_PAIRS, :], in_=residual_bias.rearrange("(h n) -> h n", h=O_PAIRS)
-        )
         coef_sb = []
         for h in range(O_PAIRS):
             coef_h = coef_pool.tile([P, 2, K], BF16, name="coef_h")
@@ -69,6 +61,15 @@ def tile_bsplinebasis_v2_s_kernel(
                 ),
             )
             coef_sb.append(coef_h)
+            if h == 0:
+                nc.sync.dma_start(
+                    out=rw_sb[:].rearrange("p (h t) i -> p h (t i)", t=2),
+                    in_=residual_weight.rearrange("(h p t) i -> p h (t i)", p=P, t=2),
+                )
+                nc.sync.dma_start(
+                    out=bias_rows[0:O_PAIRS, :],
+                    in_=residual_bias.rearrange("(h n) -> h n", h=O_PAIRS),
+                )
 
         zero_col = const.tile([P, 1], F32)
         nc.vector.memset(zero_col[:], 0.0)
@@ -110,7 +111,7 @@ def tile_bsplinebasis_v2_s_kernel(
                 op0=ALU.max,
                 op1=ALU.min,
             )
-            u_g = psum_u.tile([P, 2, P], BF16, name="u_g")
+            u_g = psum_s.tile([P, 2, P], BF16, name="u_g", tag="s")
             for u in range(2):
                 first = g * half + u * (half // 2)
                 nc.tensor.transpose(
@@ -120,21 +121,50 @@ def tile_bsplinebasis_v2_s_kernel(
                 )
             u_ps.append(u_g)
 
-        xT_ps = psum_mx.tile([P, P], BF16, tag="mx")
-        nc.tensor.transpose(xT_ps[:], x_sb[:], ident_bf[:])
+        small_ps = psum_s.tile([P, 2, P], F32, tag="s")
+        xT_ps = small_ps[:, 0, 0 : P // 2].bitcast(BF16)
+        nc.tensor.transpose(xT_ps, x_sb[:], ident_bf[:])
         xT_sb = keep.tile([P, P], BF16)
-        nc.vector.tensor_copy(out=xT_sb[:], in_=xT_ps[:])
+        nc.vector.tensor_copy(out=xT_sb[:], in_=xT_ps)
 
         base_sum = keep.tile([P, O_TILES], F32)
         nc.vector.tensor_reduce(out=base_sum[:], in_=base_sb[:], axis=AX.X, op=ALU.add)
         scale_col = keep.tile([P, O_TILES], F32)
         nc.vector.tensor_scalar_mul(out=scale_col[:], in0=base_sum[:], scalar1=1.0 / P)
 
-        rwT_ps = psum_t.tile([P, O_TILES, P], BF16, tag="t")
+        coef_codes = keep.tile([P, O_TILES, PASSES * P], U32, align_bytes=64)
+        coef_scales = keep.tile([P, O_TILES, PASSES * P], U8, align_bytes=64)
+        words_ps = {}
+
+        def transpose_tile(c):
+            coef_words = coef_sb[c // 2][:, c % 2, :].bitcast(F32)
+            words_c = psum_t.tile([P, 2 * PASSES, P], F32, name="words_c", tag="t")
+            for m in range(2 * PASSES):
+                nc.tensor.transpose(
+                    words_c[:, m, :], coef_words[:, m * P : (m + 1) * P], ident_f32[:]
+                )
+            words_ps[c] = words_c
+
+        def regroup_and_quantise(c):
+            grouped = group_pool.tile([P, PASSES, P, 4], BF16, align_bytes=64)
+            nc.scalar.copy(
+                out=grouped[:].bitcast(F32),
+                in_=words_ps[c][:].rearrange("p (g u) o -> p g o u", u=2),
+            )
+            nc.vector.quantize_mx(
+                out=coef_codes[:, c, :].bitcast(FP8X4),
+                scales=coef_scales[:, c, :],
+                in_=grouped[:].rearrange("p g o t -> p (g o t)"),
+            )
+
+        transpose_tile(0)
+        transpose_tile(1)
+        rwT_ps = psum_s.tile([P, O_TILES, P], BF16, tag="s")
         for c in range(O_TILES):
             nc.tensor.transpose(rwT_ps[:, c, :], rw_sb[:, c, :], ident_bf[:])
-        bias_ps = psum_mx.tile([P, P], F32, tag="mx")
-        nc.tensor.transpose(bias_ps[:], bias_rows[:].bitcast(F32), ident_f32[:])
+        nc.tensor.transpose(small_ps[:, 1, :], bias_rows[:].bitcast(F32), ident_f32[:])
+        transpose_tile(2)
+        transpose_tile(3)
         rwT_sb = keep.tile([P, O_TILES, P], BF16)
         bias_col = keep.tile([P, O_TILES], F32)
 
@@ -186,7 +216,7 @@ def tile_bsplinebasis_v2_s_kernel(
             if g == 0:
                 nc.vector.tensor_copy(out=rwT_sb[:], in_=rwT_ps[:])
                 nc.vector.tensor_copy(
-                    out=bias_col[:], in_=bias_ps[:, 0:O_PAIRS].bitcast(BF16)
+                    out=bias_col[:], in_=small_ps[:, 1, 0:O_PAIRS].bitcast(BF16)
                 )
             nc.vector.quantize_mx(
                 out=basis_codes[:, g, :].bitcast(FP8X4),
@@ -194,63 +224,65 @@ def tile_bsplinebasis_v2_s_kernel(
                 in_=basis_bf[:].rearrange("p n e -> p (n e)"),
             )
 
-        coef_codes = keep.tile([P, O_TILES, PASSES * P], U32, align_bytes=64)
-        coef_scales = keep.tile([P, O_TILES, PASSES * P], U8, align_bytes=64)
         for c in range(O_TILES):
-            coef_words = coef_sb[c // 2][:, c % 2, :].bitcast(F32)
-            words_ps = psum_t.tile([P, 2 * PASSES, P], F32, tag="t")
-            for m in range(2 * PASSES):
-                nc.tensor.transpose(
-                    words_ps[:, m, :], coef_words[:, m * P : (m + 1) * P], ident_f32[:]
-                )
-            grouped = group_pool.tile([P, PASSES, P, 4], BF16, align_bytes=64)
-            nc.scalar.copy(
-                out=grouped[:].bitcast(F32),
-                in_=words_ps[:].rearrange("p (g u) o -> p g o u", u=2),
-            )
-            nc.vector.quantize_mx(
-                out=coef_codes[:, c, :].bitcast(FP8X4),
-                scales=coef_scales[:, c, :],
-                in_=grouped[:].rearrange("p g o t -> p (g o t)"),
-            )
+            regroup_and_quantise(c)
+            if c + PER_BANK < O_TILES:
+                transpose_tile(c + PER_BANK)
 
         spline_ps = []
-        for c in range(O_TILES):
-            if c % PER_BANK == 0:
-                spline_bank = psum_mx.tile([P, PER_BANK, P], F32, tag="mx")
-                spline_ps.append(spline_bank)
-            for g in range(PASSES):
-                cols = slice(g * P, (g + 1) * P)
-                nc.tensor.matmul_mx(
-                    out=spline_ps[c // PER_BANK][:, c % PER_BANK, :],
-                    lhsT=coef_codes[:, c, cols].bitcast(FP8X4),
-                    lhsT_scale=coef_scales[:, c, cols],
-                    rhs=basis_codes[:, g, :].bitcast(FP8X4),
-                    rhs_scale=basis_scales[:, g, :],
-                    start=(g == 0),
-                    stop=(g == PASSES - 1),
-                )
-
+        out_ps = []
         for h in range(O_PAIRS):
-            out_ps = psum_t.tile([P, 2, P], F32, tag="t")
+            spline_h = psum_s.tile([P, 2, P], F32, name="spline_h", tag="s")
+            for t in range(2):
+                c = 2 * h + t
+                for g in range(PASSES):
+                    cols = slice(g * P, (g + 1) * P)
+                    nc.tensor.matmul_mx(
+                        out=spline_h[:, t, :],
+                        lhsT=coef_codes[:, c, cols].bitcast(FP8X4),
+                        lhsT_scale=coef_scales[:, c, cols],
+                        rhs=basis_codes[:, g, :].bitcast(FP8X4),
+                        rhs_scale=basis_scales[:, g, :],
+                        start=(g == 0),
+                        stop=(g == PASSES - 1),
+                    )
+            spline_ps.append(spline_h)
+            out_h = psum_t.tile([P, 2, P], F32, name="out_h", tag="t")
+            nc.tensor.matmul(
+                out=out_h[:].rearrange("b t p -> b (t p)"),
+                lhsT=xT_sb[:],
+                rhs=rwT_sb[:, 2 * h : 2 * h + 2, :].rearrange("i c p -> i (c p)"),
+                start=True,
+                stop=False,
+            )
+            out_ps.append(out_h)
+
+        served_in_turn = [h for first in range(O_PAIRS // 2) for h in (first, first + O_PAIRS // 2)]
+        for h in served_in_turn:
             for t in range(2):
                 c = 2 * h + t
                 scaled = stage.tile([P, P], F32)
-                nc.scalar.activation(
-                    out=scaled[:], in_=spline_ps[c // PER_BANK][:, c % PER_BANK, :],
-                    func=ACT.Identity,
-                    scale=scale_col[:, c : c + 1], bias=bias_col[:, c : c + 1],
-                )
+                if h < O_PAIRS // 2:
+                    nc.scalar.activation(
+                        out=scaled[:], in_=spline_ps[h][:, t, :], func=ACT.Identity,
+                        scale=scale_col[:, c : c + 1], bias=bias_col[:, c : c + 1],
+                    )
+                else:
+                    nc.vector.tensor_scalar(
+                        out=scaled[:], in0=spline_ps[h][:, t, :],
+                        scalar1=scale_col[:, c : c + 1], scalar2=bias_col[:, c : c + 1],
+                        op0=ALU.mult, op1=ALU.add,
+                    )
                 nc.tensor.matmul(
-                    out=out_ps[:, t, :], lhsT=xT_sb[:], rhs=rwT_sb[:, c, :],
-                    start=True, stop=False,
+                    out=out_ps[h][:, t, :], lhsT=scaled[:], rhs=ident_f32[:],
+                    is_transpose=True, start=False, stop=(t == 1),
                 )
-                nc.tensor.matmul(
-                    out=out_ps[:, t, :], lhsT=scaled[:], rhs=ident_f32[:],
-                    is_transpose=True, start=False, stop=True,
-                )
+        for h in served_in_turn:
             out_sb = stage.tile([P, P, 2], F32)
-            nc.vector.tensor_copy(out=out_sb[:], in_=out_ps[:].rearrange("b t p -> b p t"))
+            if h < O_PAIRS // 2:
+                nc.scalar.copy(out=out_sb[:], in_=out_ps[h][:].rearrange("b t p -> b p t"))
+            else:
+                nc.vector.tensor_copy(out=out_sb[:], in_=out_ps[h][:].rearrange("b t p -> b p t"))
             nc.sync.dma_start(
                 out=out[:, 2 * h * P : 2 * (h + 1) * P],
                 in_=out_sb[:].rearrange("b p t -> b (p t)"),

@@ -125,7 +125,6 @@ def tile_bsplinebasis_v2_s_kernel(
         xT_ps = small_ps[:, 0, 0 : P // 2].bitcast(BF16)
         nc.tensor.transpose(xT_ps, x_sb[:], ident_bf[:])
         xT_sb = keep.tile([P, P], BF16)
-        nc.vector.tensor_copy(out=xT_sb[:], in_=xT_ps)
 
         base_sum = keep.tile([P, O_TILES], F32)
         nc.vector.tensor_reduce(out=base_sum[:], in_=base_sb[:], axis=AX.X, op=ALU.add)
@@ -172,6 +171,15 @@ def tile_bsplinebasis_v2_s_kernel(
         basis_scales = keep.tile([P, PASSES, P], U8, align_bytes=64)
         root_sixth = 1.0 / math.sqrt(6.0)
         root_two_thirds = math.sqrt(2.0 / 3.0)
+        basis_bf = []
+
+        def quantise_basis(g):
+            nc.vector.quantize_mx(
+                out=basis_codes[:, g, :].bitcast(FP8X4),
+                scales=basis_scales[:, g, :],
+                in_=basis_bf[g][:].rearrange("p n e -> p (n e)"),
+            )
+
         for g in range(PASSES):
             dist = work.tile([P, 2, 2 * P], F32)
             for e in range(2):
@@ -182,50 +190,46 @@ def tile_bsplinebasis_v2_s_kernel(
                     scale=2.5,
                     bias=centre[:, e : e + 1],
                 )
-            wide_sq = work.tile([P, 2, 2 * P], F32)
+            dist_bue = dist[:].rearrange("p e n -> p n e")
+            wide_sq = work.tile([P, 2 * P, 2], F32)
             nc.scalar.activation(
-                out=wide_sq[:], in_=dist[:], func=ACT.Square,
+                out=wide_sq[:], in_=dist_bue, func=ACT.Square,
                 scale=root_sixth, bias=-2.0 * root_sixth,
             )
-            narrow_sq = work.tile([P, 2, 2 * P], F32)
+            narrow_sq = work.tile([P, 2 * P, 2], F32)
             nc.scalar.activation(
-                out=narrow_sq[:], in_=dist[:], func=ACT.Square,
+                out=narrow_sq[:], in_=dist_bue, func=ACT.Square,
                 scale=root_two_thirds, bias=-root_two_thirds,
             )
-            wide_cube = work.tile([P, 2, 2 * P], F32)
+            wide_cube = work.tile([P, 2 * P, 2], F32)
             nc.vector.scalar_tensor_tensor(
-                out=wide_cube[:], in0=dist[:], scalar=2.0, in1=wide_sq[:],
+                out=wide_cube[:], in0=dist_bue, scalar=2.0, in1=wide_sq[:],
                 op0=ALU.subtract, op1=ALU.mult,
             )
-            narrow_cube = work.tile([P, 2, 2 * P], F32)
+            narrow_cube = work.tile([P, 2 * P, 2], F32)
             nc.vector.scalar_tensor_tensor(
-                out=narrow_cube[:], in0=dist[:], scalar=1.0, in1=narrow_sq[:],
+                out=narrow_cube[:], in0=dist_bue, scalar=1.0, in1=narrow_sq[:],
                 op0=ALU.subtract, op1=ALU.mult,
             )
-            wide_cut = work.tile([P, 2, 2 * P], F32)
+            wide_cut = work.tile([P, 2 * P, 2], F32)
             nc.vector.tensor_scalar_min(out=wide_cut[:], in0=wide_cube[:], scalar1=0.0)
-            basis_bf = work.tile([P, 2 * P, 2], BF16, align_bytes=64)
+            if g > 0:
+                quantise_basis(g - 1)
+            basis_g = work.tile([P, 2 * P, 2], BF16, align_bytes=64)
             nc.vector.scalar_tensor_tensor(
-                out=basis_bf[:],
-                in0=narrow_cube[:].rearrange("p e n -> p n e"),
-                scalar=0.0,
-                in1=wide_cut[:].rearrange("p e n -> p n e"),
-                op0=ALU.min,
-                op1=ALU.subtract,
+                out=basis_g[:], in0=narrow_cube[:], scalar=0.0, in1=wide_cut[:],
+                op0=ALU.min, op1=ALU.subtract,
             )
-            if g == 0:
-                nc.vector.tensor_copy(out=rwT_sb[:], in_=rwT_ps[:])
-                nc.vector.tensor_copy(
-                    out=bias_col[:], in_=small_ps[:, 1, 0:O_PAIRS].bitcast(BF16)
-                )
-            nc.vector.quantize_mx(
-                out=basis_codes[:, g, :].bitcast(FP8X4),
-                scales=basis_scales[:, g, :],
-                in_=basis_bf[:].rearrange("p n e -> p (n e)"),
-            )
+            basis_bf.append(basis_g)
+
+        nc.scalar.copy(out=xT_sb[:], in_=xT_ps)
+        nc.scalar.copy(out=rwT_sb[:], in_=rwT_ps[:])
+        nc.scalar.copy(out=bias_col[:], in_=small_ps[:, 1, 0:O_PAIRS].bitcast(BF16))
 
         for c in range(O_TILES):
             regroup_and_quantise(c)
+            if c == 0:
+                quantise_basis(PASSES - 1)
             if c + PER_BANK < O_TILES:
                 transpose_tile(c + PER_BANK)
 

@@ -38,8 +38,12 @@ def tile_bsplinebasis_v2_s_kernel(
         coef_pool = ctx.enter_context(tc.tile_pool(name="coef", bufs=O_PAIRS))
         group_pool = ctx.enter_context(tc.tile_pool(name="group", bufs=O_TILES))
         stage = ctx.enter_context(tc.tile_pool(name="stage", bufs=O_TILES))
-        psum_t = ctx.enter_context(tc.psum_pool(name="psum_t", bufs=4))
-        psum_s = ctx.enter_context(tc.psum_pool(name="psum_s", bufs=4))
+        psum = ctx.enter_context(tc.psum_pool(name="psum", bufs=1))
+        U_BANKS = ("b0", "b1")
+        SMALL_BANK, RW_BANK = "b2", "b3"
+        COEF_BANKS = ("b4", "b5", "b6", "b7", "b0", "b1", "b4", "b5")
+        OUT_BANKS = ("b3", "b2", "b6", "b0")
+        SPLINE_BANKS = ("b0", "b0", "b1", "b1", "b4", "b4", "b5", "b7")
 
         x_sb = keep.tile([P, P], BF16)
         nc.sync.dma_start(out=x_sb[:], in_=x)
@@ -49,6 +53,10 @@ def tile_bsplinebasis_v2_s_kernel(
             in_=scale_base.rearrange("(h p t) i -> p h (t i)", p=P, t=2),
         )
         rw_sb = keep.tile([P, O_TILES, P], BF16)
+        nc.sync.dma_start(
+            out=rw_sb[:].rearrange("p (h t) i -> p h (t i)", t=2),
+            in_=residual_weight.rearrange("(h p t) i -> p h (t i)", p=P, t=2),
+        )
         bias_rows = keep.tile([P, 2 * P], BF16)
         nc.vector.memset(bias_rows[:], 0.0)
         coef_sb = []
@@ -62,10 +70,6 @@ def tile_bsplinebasis_v2_s_kernel(
             )
             coef_sb.append(coef_h)
             if h == 0:
-                nc.sync.dma_start(
-                    out=rw_sb[:].rearrange("p (h t) i -> p h (t i)", t=2),
-                    in_=residual_weight.rearrange("(h p t) i -> p h (t i)", p=P, t=2),
-                )
                 nc.sync.dma_start(
                     out=bias_rows[0:O_PAIRS, :],
                     in_=residual_bias.rearrange("(h n) -> h n", h=O_PAIRS),
@@ -111,7 +115,7 @@ def tile_bsplinebasis_v2_s_kernel(
                 op0=ALU.max,
                 op1=ALU.min,
             )
-            u_g = psum_s.tile([P, 2, P], BF16, name="u_g", tag="s")
+            u_g = psum.tile([P, 2, P], BF16, name="u_g", tag=U_BANKS[g])
             for u in range(2):
                 first = g * half + u * (half // 2)
                 nc.tensor.transpose(
@@ -121,15 +125,8 @@ def tile_bsplinebasis_v2_s_kernel(
                 )
             u_ps.append(u_g)
 
-        small_ps = psum_s.tile([P, 2, P], F32, tag="s")
-        xT_ps = small_ps[:, 0, 0 : P // 2].bitcast(BF16)
-        nc.tensor.transpose(xT_ps, x_sb[:], ident_bf[:])
-        xT_sb = keep.tile([P, P], BF16)
-
         base_sum = keep.tile([P, O_TILES], F32)
         nc.vector.tensor_reduce(out=base_sum[:], in_=base_sb[:], axis=AX.X, op=ALU.add)
-        scale_col = keep.tile([P, O_TILES], F32)
-        nc.vector.tensor_scalar_mul(out=scale_col[:], in0=base_sum[:], scalar1=1.0 / P)
 
         coef_codes = keep.tile([P, O_TILES, PASSES * P], U32, align_bytes=64)
         coef_scales = keep.tile([P, O_TILES, PASSES * P], U8, align_bytes=64)
@@ -137,35 +134,36 @@ def tile_bsplinebasis_v2_s_kernel(
 
         def transpose_tile(c):
             coef_words = coef_sb[c // 2][:, c % 2, :].bitcast(F32)
-            words_c = psum_t.tile([P, 2 * PASSES, P], F32, name="words_c", tag="t")
+            words_c = psum.tile([P, 2 * PASSES, P], F32, name="words_c", tag=COEF_BANKS[c])
             for m in range(2 * PASSES):
                 nc.tensor.transpose(
                     words_c[:, m, :], coef_words[:, m * P : (m + 1) * P], ident_f32[:]
                 )
             words_ps[c] = words_c
 
-        def regroup_and_quantise(c):
-            grouped = group_pool.tile([P, PASSES, P, 4], BF16, align_bytes=64)
+        grouped_sb = {}
+
+        def regroup(c):
+            grouped = group_pool.tile([P, PASSES, P, 4], BF16, align_bytes=64, name="grouped")
+            grouped_sb[c] = grouped
             nc.scalar.copy(
                 out=grouped[:].bitcast(F32),
                 in_=words_ps[c][:].rearrange("p (g u) o -> p g o u", u=2),
             )
+
+        def quantise_coef(c):
             nc.vector.quantize_mx(
                 out=coef_codes[:, c, :].bitcast(FP8X4),
                 scales=coef_scales[:, c, :],
-                in_=grouped[:].rearrange("p g o t -> p (g o t)"),
+                in_=grouped_sb[c][:].rearrange("p g o t -> p (g o t)"),
             )
 
-        transpose_tile(0)
-        transpose_tile(1)
-        rwT_ps = psum_s.tile([P, O_TILES, P], BF16, tag="s")
+        rwT_ps = psum.tile([P, O_TILES, P], BF16, tag=RW_BANK)
         for c in range(O_TILES):
             nc.tensor.transpose(rwT_ps[:, c, :], rw_sb[:, c, :], ident_bf[:])
-        nc.tensor.transpose(small_ps[:, 1, :], bias_rows[:].bitcast(F32), ident_f32[:])
-        transpose_tile(2)
-        transpose_tile(3)
         rwT_sb = keep.tile([P, O_TILES, P], BF16)
         bias_col = keep.tile([P, O_TILES], F32)
+        scale_col = keep.tile([P, O_TILES], F32)
 
         basis_codes = keep.tile([P, PASSES, P], U32, align_bytes=64)
         basis_scales = keep.tile([P, PASSES, P], U8, align_bytes=64)
@@ -177,81 +175,102 @@ def tile_bsplinebasis_v2_s_kernel(
             nc.vector.quantize_mx(
                 out=basis_codes[:, g, :].bitcast(FP8X4),
                 scales=basis_scales[:, g, :],
-                in_=basis_bf[g][:].rearrange("p n e -> p (n e)"),
+                in_=basis_bf[g][:].rearrange("p b u e -> p (b u e)"),
             )
 
+        dist, wide_sq, narrow_sq, wide_cube, narrow_cube, uncut = [], [], [], [], [], []
         for g in range(PASSES):
-            dist = work.tile([P, 2, 2 * P], F32)
+            dist.append(work.tile([P, 2, P, 2], F32, name="dist"))
+            wide_sq.append(work.tile([P, P, 2, 2], F32, name="wide_sq"))
+            narrow_sq.append(work.tile([P, P, 2, 2], F32, name="narrow_sq"))
+            wide_cube.append(work.tile([P, P, 2, 2], F32, name="wide_cube"))
+            narrow_cube.append(work.tile([P, P, 2, 2], F32, name="narrow_cube"))
+            uncut.append(work.tile([P, P, 2, 2], BF16, name="uncut"))
+            basis_bf.append(work.tile([P, P, 2, 2], BF16, align_bytes=64, name="basis_g"))
+
+        def flat(ap):
+            return ap.rearrange("p b u e -> p (b u) e")
+
+        def dist_view(g, bs):
+            return dist[g][:, :, bs, :].rearrange("p e b u -> p (b u) e")
+
+        def squares(g, bs):
             for e in range(2):
                 nc.scalar.activation(
-                    out=dist[:, e, :].rearrange("p (b u) -> p b u", u=2),
-                    in_=u_ps[g][:].rearrange("p u b -> p b u"),
-                    func=ACT.Abs,
-                    scale=2.5,
-                    bias=centre[:, e : e + 1],
+                    out=dist[g][:, e, bs, :], in_=u_ps[g][:, :, bs].rearrange("p u b -> p b u"),
+                    func=ACT.Abs, scale=2.5, bias=centre[:, e : e + 1],
                 )
-            dist_bue = dist[:].rearrange("p e n -> p n e")
-            wide_sq = work.tile([P, 2 * P, 2], F32)
             nc.scalar.activation(
-                out=wide_sq[:], in_=dist_bue, func=ACT.Square,
+                out=flat(wide_sq[g][:, bs]), in_=dist_view(g, bs), func=ACT.Square,
                 scale=root_sixth, bias=-2.0 * root_sixth,
             )
-            narrow_sq = work.tile([P, 2 * P, 2], F32)
             nc.scalar.activation(
-                out=narrow_sq[:], in_=dist_bue, func=ACT.Square,
+                out=flat(narrow_sq[g][:, bs]), in_=dist_view(g, bs), func=ACT.Square,
                 scale=root_two_thirds, bias=-root_two_thirds,
             )
-            wide_cube = work.tile([P, 2 * P, 2], F32)
+
+        def cube(out, centre_at, g, bs, sq):
             nc.vector.scalar_tensor_tensor(
-                out=wide_cube[:], in0=dist_bue, scalar=2.0, in1=wide_sq[:],
-                op0=ALU.subtract, op1=ALU.mult,
+                out=flat(out[:, bs]), in0=dist_view(g, bs),
+                scalar=centre_at, in1=flat(sq[:, bs]), op0=ALU.subtract, op1=ALU.mult,
             )
-            narrow_cube = work.tile([P, 2 * P, 2], F32)
+
+        def combine(g):
             nc.vector.scalar_tensor_tensor(
-                out=narrow_cube[:], in0=dist_bue, scalar=1.0, in1=narrow_sq[:],
-                op0=ALU.subtract, op1=ALU.mult,
-            )
-            wide_cut = work.tile([P, 2 * P, 2], F32)
-            nc.vector.tensor_scalar_min(out=wide_cut[:], in0=wide_cube[:], scalar1=0.0)
-            if g > 0:
-                quantise_basis(g - 1)
-            basis_g = work.tile([P, 2 * P, 2], BF16, align_bytes=64)
-            nc.vector.scalar_tensor_tensor(
-                out=basis_g[:], in0=narrow_cube[:], scalar=0.0, in1=wide_cut[:],
+                out=flat(uncut[g][:]), in0=flat(narrow_cube[g][:]),
+                scalar=0.0, in1=flat(wide_cube[g][:]),
                 op0=ALU.min, op1=ALU.subtract,
             )
-            basis_bf.append(basis_g)
 
-        nc.scalar.copy(out=xT_sb[:], in_=xT_ps)
-        nc.scalar.copy(out=rwT_sb[:], in_=rwT_ps[:])
-        nc.scalar.copy(out=bias_col[:], in_=small_ps[:, 1, 0:O_PAIRS].bitcast(BF16))
+        def cut(g):
+            nc.vector.tensor_scalar_max(
+                out=basis_bf[g][:].rearrange("p b u e -> p (b u e)"),
+                in0=uncut[g][:].rearrange("p b u e -> p (b u e)"), scalar1=0.0,
+            )
 
+        first_half, second_half, both = slice(0, P // 2), slice(P // 2, P), slice(0, P)
+        squares(0, first_half)
+        squares(0, second_half)
+        squares(1, both)
+
+        cube(wide_cube[0], 2.0, 0, first_half, wide_sq[0])
+        cube(narrow_cube[0], 1.0, 0, first_half, narrow_sq[0])
+        nc.vector.tensor_scalar_mul(out=scale_col[:], in0=base_sum[:], scalar1=1.0 / P)
+        nc.vector.tensor_copy(out=rwT_sb[:], in_=rwT_ps[:])
+        cube(wide_cube[0], 2.0, 0, second_half, wide_sq[0])
+        cube(narrow_cube[0], 1.0, 0, second_half, narrow_sq[0])
+        combine(0)
+        cut(0)
+        cube(wide_cube[1], 2.0, 1, both, wide_sq[1])
+        quantise_basis(0)
+        cube(narrow_cube[1], 1.0, 1, both, narrow_sq[1])
+        combine(1)
+
+        small_ps = psum.tile([P, 2, P], F32, tag=SMALL_BANK)
+        xT_ps = small_ps[:, 0, 0 : P // 2].bitcast(BF16)
+        nc.tensor.transpose(xT_ps, x_sb[:], ident_bf[:])
+        xT_sb = keep.tile([P, P], BF16)
+
+        nc.tensor.transpose(small_ps[:, 1, :], bias_rows[:].bitcast(F32), ident_f32[:])
+        for c in range(6):
+            transpose_tile(c)
         for c in range(O_TILES):
-            regroup_and_quantise(c)
-            if c == 0:
-                quantise_basis(PASSES - 1)
-            if c + PER_BANK < O_TILES:
-                transpose_tile(c + PER_BANK)
+            regroup(c)
+            if c + 6 < O_TILES:
+                transpose_tile(c + 6)
+        nc.scalar.copy(out=xT_sb[:], in_=xT_ps)
+        nc.scalar.copy(out=bias_col[:], in_=small_ps[:, 1, 0:O_PAIRS].bitcast(BF16))
+        quantise_coef(0)
+        cut(1)
+        quantise_coef(1)
+        quantise_basis(1)
+        for c in range(2, O_TILES):
+            quantise_coef(c)
 
-        spline_ps = []
-        out_ps = []
-        for h in range(O_PAIRS):
-            spline_h = psum_s.tile([P, 2, P], F32, name="spline_h", tag="s")
-            for t in range(2):
-                c = 2 * h + t
-                for g in range(PASSES):
-                    cols = slice(g * P, (g + 1) * P)
-                    nc.tensor.matmul_mx(
-                        out=spline_h[:, t, :],
-                        lhsT=coef_codes[:, c, cols].bitcast(FP8X4),
-                        lhsT_scale=coef_scales[:, c, cols],
-                        rhs=basis_codes[:, g, :].bitcast(FP8X4),
-                        rhs_scale=basis_scales[:, g, :],
-                        start=(g == 0),
-                        stop=(g == PASSES - 1),
-                    )
-            spline_ps.append(spline_h)
-            out_h = psum_t.tile([P, 2, P], F32, name="out_h", tag="t")
+        out_ps = {}
+
+        def open_pair(h):
+            out_h = psum.tile([P, 2, P], F32, name="out_h", tag=OUT_BANKS[h])
             nc.tensor.matmul(
                 out=out_h[:].rearrange("b t p -> b (t p)"),
                 lhsT=xT_sb[:],
@@ -259,35 +278,79 @@ def tile_bsplinebasis_v2_s_kernel(
                 start=True,
                 stop=False,
             )
-            out_ps.append(out_h)
+            out_ps[h] = out_h
 
-        served_in_turn = [h for first in range(O_PAIRS // 2) for h in (first, first + O_PAIRS // 2)]
-        for h in served_in_turn:
+        spline_ps = {}
+        scaled_sb = {}
+
+        def multiply(tiles):
+            spline = psum.tile([P, len(tiles), P], F32, name="spline", tag=SPLINE_BANKS[tiles[0]])
+            for n, c in enumerate(tiles):
+                for g in range(PASSES):
+                    cols = slice(g * P, (g + 1) * P)
+                    nc.tensor.matmul_mx(
+                        out=spline[:, n, :],
+                        lhsT=coef_codes[:, c, cols].bitcast(FP8X4),
+                        lhsT_scale=coef_scales[:, c, cols],
+                        rhs=basis_codes[:, g, :].bitcast(FP8X4),
+                        rhs_scale=basis_scales[:, g, :],
+                        start=(g == 0),
+                        stop=(g == PASSES - 1),
+                    )
+                spline_ps[c] = spline[:, n, :]
+
+        def scale_tile(c, on_scalar):
+            scaled = stage.tile([P, P], F32, name="scaled")
+            if on_scalar:
+                nc.scalar.activation(
+                    out=scaled[:], in_=spline_ps[c], func=ACT.Identity,
+                    scale=scale_col[:, c : c + 1], bias=bias_col[:, c : c + 1],
+                )
+            else:
+                nc.vector.tensor_scalar(
+                    out=scaled[:], in0=spline_ps[c],
+                    scalar1=scale_col[:, c : c + 1], scalar2=bias_col[:, c : c + 1],
+                    op0=ALU.mult, op1=ALU.add,
+                )
+            scaled_sb[c] = scaled
+
+        def add_pair(h):
             for t in range(2):
-                c = 2 * h + t
-                scaled = stage.tile([P, P], F32)
-                if h < O_PAIRS // 2:
-                    nc.scalar.activation(
-                        out=scaled[:], in_=spline_ps[h][:, t, :], func=ACT.Identity,
-                        scale=scale_col[:, c : c + 1], bias=bias_col[:, c : c + 1],
-                    )
-                else:
-                    nc.vector.tensor_scalar(
-                        out=scaled[:], in0=spline_ps[h][:, t, :],
-                        scalar1=scale_col[:, c : c + 1], scalar2=bias_col[:, c : c + 1],
-                        op0=ALU.mult, op1=ALU.add,
-                    )
                 nc.tensor.matmul(
-                    out=out_ps[h][:, t, :], lhsT=scaled[:], rhs=ident_f32[:],
+                    out=out_ps[h][:, t, :], lhsT=scaled_sb[2 * h + t][:], rhs=ident_f32[:],
                     is_transpose=True, start=False, stop=(t == 1),
                 )
-        for h in served_in_turn:
-            out_sb = stage.tile([P, P, 2], F32)
-            if h < O_PAIRS // 2:
-                nc.scalar.copy(out=out_sb[:], in_=out_ps[h][:].rearrange("b t p -> b p t"))
-            else:
-                nc.vector.tensor_copy(out=out_sb[:], in_=out_ps[h][:].rearrange("b t p -> b p t"))
+
+        def store_pair(h, copy):
+            out_sb = stage.tile([P, P, 2], F32, name="out_sb")
+            copy(out=out_sb[:], in_=out_ps[h][:].rearrange("b t p -> b p t"))
             nc.sync.dma_start(
                 out=out[:, 2 * h * P : 2 * (h + 1) * P],
                 in_=out_sb[:].rearrange("b p t -> b (p t)"),
             )
+
+        multiply((0, 1))
+        multiply((2, 3))
+        multiply((4, 5))
+        multiply((6,))
+        open_pair(0)
+        open_pair(2)
+        scale_tile(0, True)
+        scale_tile(1, True)
+        scale_tile(4, False)
+        scale_tile(5, False)
+        multiply((7,))
+        add_pair(0)
+        open_pair(1)
+        open_pair(3)
+        scale_tile(2, True)
+        scale_tile(3, True)
+        scale_tile(6, False)
+        add_pair(2)
+        store_pair(0, nc.vector.tensor_copy)
+        add_pair(1)
+        scale_tile(7, True)
+        add_pair(3)
+        store_pair(2, nc.vector.tensor_copy)
+        store_pair(1, nc.scalar.copy)
+        store_pair(3, nc.vector.tensor_copy)

@@ -42,11 +42,17 @@ def tile_bsplinebasis_v2_s_kernel(
         U_BANKS = ("b0", "b1")
         SMALL_BANK, RW_BANK = "b2", "b3"
         COEF_BANKS = ("b4", "b5", "b6", "b7", "b0", "b1", "b4", "b5")
-        OUT_BANKS = ("b3", "b2", "b6", "b0")
-        SPLINE_BANKS = ("b0", "b0", "b1", "b1", "b4", "b4", "b5", "b7")
+        OUT_BANKS = ("b3", "b2", "b6", "b7")
+        SPLINE_BANKS = ("b0", "b0", "b1", "b1", "b4", "b4", "b4", "b5")
 
         x_sb = keep.tile([P, P], BF16)
         nc.sync.dma_start(out=x_sb[:], in_=x)
+        bias_rows = keep.tile([P, 2 * P], BF16)
+        nc.vector.memset(bias_rows[:], 0.0)
+        nc.sync.dma_start(
+            out=bias_rows[0:O_PAIRS, :],
+            in_=residual_bias.rearrange("(h n) -> h n", h=O_PAIRS),
+        )
         base_sb = keep.tile([P, O_TILES, P], BF16)
         nc.sync.dma_start(
             out=base_sb[:].rearrange("p (h t) i -> p h (t i)", t=2),
@@ -57,8 +63,6 @@ def tile_bsplinebasis_v2_s_kernel(
             out=rw_sb[:].rearrange("p (h t) i -> p h (t i)", t=2),
             in_=residual_weight.rearrange("(h p t) i -> p h (t i)", p=P, t=2),
         )
-        bias_rows = keep.tile([P, 2 * P], BF16)
-        nc.vector.memset(bias_rows[:], 0.0)
         coef_sb = []
         for h in range(O_PAIRS):
             coef_h = coef_pool.tile([P, 2, K], BF16, name="coef_h")
@@ -69,11 +73,6 @@ def tile_bsplinebasis_v2_s_kernel(
                 ),
             )
             coef_sb.append(coef_h)
-            if h == 0:
-                nc.sync.dma_start(
-                    out=bias_rows[0:O_PAIRS, :],
-                    in_=residual_bias.rearrange("(h n) -> h n", h=O_PAIRS),
-                )
 
         zero_col = const.tile([P, 1], F32)
         nc.vector.memset(zero_col[:], 0.0)
@@ -103,6 +102,11 @@ def tile_bsplinebasis_v2_s_kernel(
             )
 
         half = P // PASSES
+        small_ps = psum.tile([P, 2, P], F32, tag=SMALL_BANK)
+        xT_ps = small_ps[:, 0, 0 : P // 2].bitcast(BF16)
+        nc.tensor.transpose(xT_ps, x_sb[:], ident_bf[:])
+        xT_sb = keep.tile([P, P], BF16)
+        nc.scalar.copy(out=xT_sb[:], in_=xT_ps)
         clamped = keep.tile([P, P, 4], BF16)
         u_ps = []
         for g in range(PASSES):
@@ -124,6 +128,8 @@ def tile_bsplinebasis_v2_s_kernel(
                     ident_bf[:],
                 )
             u_ps.append(u_g)
+
+        nc.tensor.transpose(small_ps[:, 1, :], bias_rows[:].bitcast(F32), ident_f32[:])
 
         base_sum = keep.tile([P, O_TILES], F32)
         nc.vector.tensor_reduce(out=base_sum[:], in_=base_sb[:], axis=AX.X, op=ALU.add)
@@ -232,40 +238,20 @@ def tile_bsplinebasis_v2_s_kernel(
         squares(0, first_half)
         squares(0, second_half)
         squares(1, both)
+        nc.scalar.copy(out=bias_col[:], in_=small_ps[:, 1, 0:O_PAIRS].bitcast(BF16))
 
         cube(wide_cube[0], 2.0, 0, first_half, wide_sq[0])
         cube(narrow_cube[0], 1.0, 0, first_half, narrow_sq[0])
-        nc.vector.tensor_scalar_mul(out=scale_col[:], in0=base_sum[:], scalar1=1.0 / P)
         nc.vector.tensor_copy(out=rwT_sb[:], in_=rwT_ps[:])
         cube(wide_cube[0], 2.0, 0, second_half, wide_sq[0])
         cube(narrow_cube[0], 1.0, 0, second_half, narrow_sq[0])
+        nc.vector.tensor_scalar_mul(out=scale_col[:], in0=base_sum[:], scalar1=1.0 / P)
         combine(0)
-        cut(0)
         cube(wide_cube[1], 2.0, 1, both, wide_sq[1])
-        quantise_basis(0)
+        cut(0)
         cube(narrow_cube[1], 1.0, 1, both, narrow_sq[1])
+        quantise_basis(0)
         combine(1)
-
-        small_ps = psum.tile([P, 2, P], F32, tag=SMALL_BANK)
-        xT_ps = small_ps[:, 0, 0 : P // 2].bitcast(BF16)
-        nc.tensor.transpose(xT_ps, x_sb[:], ident_bf[:])
-        xT_sb = keep.tile([P, P], BF16)
-
-        nc.tensor.transpose(small_ps[:, 1, :], bias_rows[:].bitcast(F32), ident_f32[:])
-        for c in range(6):
-            transpose_tile(c)
-        for c in range(O_TILES):
-            regroup(c)
-            if c + 6 < O_TILES:
-                transpose_tile(c + 6)
-        nc.scalar.copy(out=xT_sb[:], in_=xT_ps)
-        nc.scalar.copy(out=bias_col[:], in_=small_ps[:, 1, 0:O_PAIRS].bitcast(BF16))
-        quantise_coef(0)
-        cut(1)
-        quantise_coef(1)
-        quantise_basis(1)
-        for c in range(2, O_TILES):
-            quantise_coef(c)
 
         out_ps = {}
 
@@ -279,6 +265,23 @@ def tile_bsplinebasis_v2_s_kernel(
                 stop=False,
             )
             out_ps[h] = out_h
+
+        for c in range(6):
+            transpose_tile(c)
+        open_pair(0)
+        open_pair(1)
+        for c in range(O_TILES):
+            regroup(c)
+            if c + 6 < O_TILES:
+                transpose_tile(c + 6)
+        open_pair(2)
+        open_pair(3)
+        quantise_coef(0)
+        cut(1)
+        quantise_coef(1)
+        quantise_basis(1)
+        for c in range(2, O_TILES):
+            quantise_coef(c)
 
         spline_ps = {}
         scaled_sb = {}
@@ -331,18 +334,13 @@ def tile_bsplinebasis_v2_s_kernel(
 
         multiply((0, 1))
         multiply((2, 3))
-        multiply((4, 5))
-        multiply((6,))
-        open_pair(0)
-        open_pair(2)
+        multiply((4, 5, 6))
+        multiply((7,))
         scale_tile(0, True)
         scale_tile(1, True)
         scale_tile(4, False)
         scale_tile(5, False)
-        multiply((7,))
         add_pair(0)
-        open_pair(1)
-        open_pair(3)
         scale_tile(2, True)
         scale_tile(3, True)
         scale_tile(6, False)

@@ -43,16 +43,12 @@ def tile_bsplinebasis_v2_s_kernel(
         SMALL_BANK, RW_BANK = "b2", "b3"
         COEF_BANKS = ("b4", "b5", "b6", "b7", "b0", "b1", "b4", "b5")
         OUT_BANKS = ("b3", "b2", "b6", "b7")
-        SPLINE_BANKS = ("b0", "b0", "b1", "b1", "b4", "b4", "b4", "b5")
+        SPLINE_BANKS = ("b0", "b0", "b0", "b0", "b1", "b1", "b4", "b5")
 
         x_sb = keep.tile([P, P], BF16)
         nc.sync.dma_start(out=x_sb[:], in_=x)
         bias_rows = keep.tile([P, 2 * P], BF16)
         nc.vector.memset(bias_rows[:], 0.0)
-        nc.sync.dma_start(
-            out=bias_rows[0:O_PAIRS, :],
-            in_=residual_bias.rearrange("(h n) -> h n", h=O_PAIRS),
-        )
         base_sb = keep.tile([P, O_TILES, P], BF16)
         nc.sync.dma_start(
             out=base_sb[:].rearrange("p (h t) i -> p h (t i)", t=2),
@@ -62,6 +58,10 @@ def tile_bsplinebasis_v2_s_kernel(
         nc.sync.dma_start(
             out=rw_sb[:].rearrange("p (h t) i -> p h (t i)", t=2),
             in_=residual_weight.rearrange("(h p t) i -> p h (t i)", p=P, t=2),
+        )
+        nc.sync.dma_start(
+            out=bias_rows[0:O_PAIRS, :],
+            in_=residual_bias.rearrange("(h n) -> h n", h=O_PAIRS),
         )
         coef_sb = []
         for h in range(O_PAIRS):
@@ -102,7 +102,7 @@ def tile_bsplinebasis_v2_s_kernel(
             )
 
         half = P // PASSES
-        small_ps = psum.tile([P, 2, P], F32, tag=SMALL_BANK)
+        small_ps = psum.tile([P, 4, P], F32, tag=SMALL_BANK)
         xT_ps = small_ps[:, 0, 0 : P // 2].bitcast(BF16)
         nc.tensor.transpose(xT_ps, x_sb[:], ident_bf[:])
         xT_sb = keep.tile([P, P], BF16)
@@ -128,8 +128,6 @@ def tile_bsplinebasis_v2_s_kernel(
                     ident_bf[:],
                 )
             u_ps.append(u_g)
-
-        nc.tensor.transpose(small_ps[:, 1, :], bias_rows[:].bitcast(F32), ident_f32[:])
 
         base_sum = keep.tile([P, O_TILES], F32)
         nc.vector.tensor_reduce(out=base_sum[:], in_=base_sb[:], axis=AX.X, op=ALU.add)
@@ -164,10 +162,12 @@ def tile_bsplinebasis_v2_s_kernel(
                 in_=grouped_sb[c][:].rearrange("p g o t -> p (g o t)"),
             )
 
-        rwT_ps = psum.tile([P, O_TILES, P], BF16, tag=RW_BANK)
+        rwT_first = psum.tile([P, O_TILES // 2, P], BF16, tag=RW_BANK)
+        rwT_ps = [rwT_first[:], small_ps[:, 2:4, :].bitcast(BF16).rearrange("i w (c p) -> i (w c) p", p=P)]
         for c in range(O_TILES):
-            nc.tensor.transpose(rwT_ps[:, c, :], rw_sb[:, c, :], ident_bf[:])
-        rwT_sb = keep.tile([P, O_TILES, P], BF16)
+            nc.tensor.transpose(rwT_ps[c // 4][:, c % 4, :], rw_sb[:, c, :], ident_bf[:])
+        nc.tensor.transpose(small_ps[:, 1, :], bias_rows[:].bitcast(F32), ident_f32[:])
+        rwT_sb = [keep.tile([P, O_TILES // 2, P], BF16, name="rwT_half%d" % n) for n in range(2)]
         bias_col = keep.tile([P, O_TILES], F32)
         scale_col = keep.tile([P, O_TILES], F32)
 
@@ -200,19 +200,17 @@ def tile_bsplinebasis_v2_s_kernel(
         def dist_view(g, bs):
             return dist[g][:, :, bs, :].rearrange("p e b u -> p (b u) e")
 
-        def squares(g, bs):
+        def distances(g):
             for e in range(2):
                 nc.scalar.activation(
-                    out=dist[g][:, e, bs, :], in_=u_ps[g][:, :, bs].rearrange("p u b -> p b u"),
+                    out=dist[g][:, e], in_=u_ps[g][:].rearrange("p u b -> p b u"),
                     func=ACT.Abs, scale=2.5, bias=centre[:, e : e + 1],
                 )
+
+        def square(out, root, centre_at, g, bs):
             nc.scalar.activation(
-                out=flat(wide_sq[g][:, bs]), in_=dist_view(g, bs), func=ACT.Square,
-                scale=root_sixth, bias=-2.0 * root_sixth,
-            )
-            nc.scalar.activation(
-                out=flat(narrow_sq[g][:, bs]), in_=dist_view(g, bs), func=ACT.Square,
-                scale=root_two_thirds, bias=-root_two_thirds,
+                out=flat(out[:, bs]), in_=dist_view(g, bs), func=ACT.Square,
+                scale=root, bias=-centre_at * root,
             )
 
         def cube(out, centre_at, g, bs, sq):
@@ -235,23 +233,30 @@ def tile_bsplinebasis_v2_s_kernel(
             )
 
         first_half, second_half, both = slice(0, P // 2), slice(P // 2, P), slice(0, P)
-        squares(0, first_half)
-        squares(0, second_half)
-        squares(1, both)
-        nc.scalar.copy(out=bias_col[:], in_=small_ps[:, 1, 0:O_PAIRS].bitcast(BF16))
+        distances(0)
+        square(wide_sq[0], root_sixth, 2.0, 0, first_half)
+        square(wide_sq[0], root_sixth, 2.0, 0, second_half)
+        square(narrow_sq[0], root_two_thirds, 1.0, 0, both)
+        distances(1)
+        square(wide_sq[1], root_sixth, 2.0, 1, both)
+        square(narrow_sq[1], root_two_thirds, 1.0, 1, both)
 
+        nc.gpsimd.tensor_scalar(
+            out=scale_col[:], in0=base_sum[:], scalar1=1.0 / P, scalar2=0.0,
+            op0=ALU.mult, op1=ALU.add,
+        )
+        nc.vector.tensor_copy(out=rwT_sb[0][:], in_=rwT_ps[0])
         cube(wide_cube[0], 2.0, 0, first_half, wide_sq[0])
-        cube(narrow_cube[0], 1.0, 0, first_half, narrow_sq[0])
-        nc.vector.tensor_copy(out=rwT_sb[:], in_=rwT_ps[:])
         cube(wide_cube[0], 2.0, 0, second_half, wide_sq[0])
-        cube(narrow_cube[0], 1.0, 0, second_half, narrow_sq[0])
-        nc.vector.tensor_scalar_mul(out=scale_col[:], in0=base_sum[:], scalar1=1.0 / P)
+        cube(narrow_cube[0], 1.0, 0, both, narrow_sq[0])
+        nc.vector.tensor_copy(out=rwT_sb[1][:], in_=rwT_ps[1])
         combine(0)
         cube(wide_cube[1], 2.0, 1, both, wide_sq[1])
         cut(0)
         cube(narrow_cube[1], 1.0, 1, both, narrow_sq[1])
         quantise_basis(0)
         combine(1)
+        nc.scalar.copy(out=bias_col[:], in_=small_ps[:, 1, 0:O_PAIRS].bitcast(BF16))
 
         out_ps = {}
 
@@ -260,7 +265,7 @@ def tile_bsplinebasis_v2_s_kernel(
             nc.tensor.matmul(
                 out=out_h[:].rearrange("b t p -> b (t p)"),
                 lhsT=xT_sb[:],
-                rhs=rwT_sb[:, 2 * h : 2 * h + 2, :].rearrange("i c p -> i (c p)"),
+                rhs=rwT_sb[h // 2][:, 2 * (h % 2) : 2 * (h % 2) + 2, :].rearrange("i c p -> i (c p)"),
                 start=True,
                 stop=False,
             )
@@ -332,23 +337,16 @@ def tile_bsplinebasis_v2_s_kernel(
                 in_=out_sb[:].rearrange("b p t -> b (p t)"),
             )
 
-        multiply((0, 1))
-        multiply((2, 3))
-        multiply((4, 5, 6))
+        multiply((0, 1, 2, 3))
+        multiply((4, 5))
+        multiply((6,))
         multiply((7,))
-        scale_tile(0, True)
-        scale_tile(1, True)
-        scale_tile(4, False)
-        scale_tile(5, False)
-        add_pair(0)
-        scale_tile(2, True)
-        scale_tile(3, True)
-        scale_tile(6, False)
-        add_pair(2)
-        store_pair(0, nc.vector.tensor_copy)
-        add_pair(1)
-        scale_tile(7, True)
-        add_pair(3)
-        store_pair(2, nc.vector.tensor_copy)
-        store_pair(1, nc.scalar.copy)
-        store_pair(3, nc.vector.tensor_copy)
+        for c in range(6):
+            scale_tile(c, True)
+        for c in (6, 7):
+            scale_tile(c, False)
+        for h in range(O_PAIRS):
+            add_pair(h)
+        for h in range(O_PAIRS - 1):
+            store_pair(h, nc.scalar.copy)
+        store_pair(O_PAIRS - 1, nc.vector.tensor_copy)

@@ -21,7 +21,7 @@ O = 1024
 O_TILES = O // P
 O_PAIRS = O_TILES // 2
 PASSES = 2
-PER_BANK = 4
+PAIRED = 6
 
 FLOPS = 2 * P * K * O + 2 * P * P * O
 
@@ -45,20 +45,24 @@ def tile_bsplinebasis_v2_s_kernel(
         OUT_BANKS = ("b3", "b2", "b6", "b7")
         SPLINE_BANKS = ("b0", "b0", "b0", "b0", "b1", "b1", "b4", "b5")
 
+        def load_rows(tile, rows):
+            nc.sync.dma_start(
+                out=tile[:, :PAIRED, :].rearrange("p (h t) i -> p h (t i)", t=2),
+                in_=rows[: PAIRED * P].rearrange("(h p t) i -> p h (t i)", p=P, t=2),
+            )
+            nc.sync.dma_start(
+                out=tile[:, PAIRED:, :],
+                in_=rows[PAIRED * P :].rearrange("(t p) i -> p t i", p=P),
+            )
+
         x_sb = keep.tile([P, P], BF16)
         nc.sync.dma_start(out=x_sb[:], in_=x)
         bias_rows = keep.tile([P, 2 * P], BF16)
         nc.vector.memset(bias_rows[:], 0.0)
         base_sb = keep.tile([P, O_TILES, P], BF16)
-        nc.sync.dma_start(
-            out=base_sb[:].rearrange("p (h t) i -> p h (t i)", t=2),
-            in_=scale_base.rearrange("(h p t) i -> p h (t i)", p=P, t=2),
-        )
+        load_rows(base_sb, scale_base)
         rw_sb = keep.tile([P, O_TILES, P], BF16)
-        nc.sync.dma_start(
-            out=rw_sb[:].rearrange("p (h t) i -> p h (t i)", t=2),
-            in_=residual_weight.rearrange("(h p t) i -> p h (t i)", p=P, t=2),
-        )
+        load_rows(rw_sb, residual_weight)
         nc.sync.dma_start(
             out=bias_rows[0:O_PAIRS, :],
             in_=residual_bias.rearrange("(h n) -> h n", h=O_PAIRS),
@@ -66,11 +70,10 @@ def tile_bsplinebasis_v2_s_kernel(
         coef_sb = []
         for h in range(O_PAIRS):
             coef_h = coef_pool.tile([P, 2, K], BF16, name="coef_h")
+            order = "(p t) i j -> p t (i j)" if 2 * h < PAIRED else "(t p) i j -> p t (i j)"
             nc.sync.dma_start(
                 out=coef_h[:],
-                in_=spline_coeffs[2 * h * P : 2 * (h + 1) * P].rearrange(
-                    "(p t) i j -> p t (i j)", t=2
-                ),
+                in_=spline_coeffs[2 * h * P : 2 * (h + 1) * P].rearrange(order, t=2),
             )
             coef_sb.append(coef_h)
 
@@ -146,20 +149,22 @@ def tile_bsplinebasis_v2_s_kernel(
             words_ps[c] = words_c
 
         grouped_sb = {}
+        whole = slice(0, PASSES)
 
-        def regroup(c):
-            grouped = group_pool.tile([P, PASSES, P, 4], BF16, align_bytes=64, name="grouped")
-            grouped_sb[c] = grouped
+        def regroup(c, gs=whole):
+            if c not in grouped_sb:
+                grouped_sb[c] = group_pool.tile([P, PASSES, P, 4], BF16, align_bytes=64, name="grouped")
             nc.scalar.copy(
-                out=grouped[:].bitcast(F32),
-                in_=words_ps[c][:].rearrange("p (g u) o -> p g o u", u=2),
+                out=grouped_sb[c][:, gs].bitcast(F32),
+                in_=words_ps[c][:, 2 * gs.start : 2 * gs.stop].rearrange("p (g u) o -> p g o u", u=2),
             )
 
-        def quantise_coef(c):
+        def quantise_coef(c, gs=whole):
+            cols = slice(gs.start * P, gs.stop * P)
             nc.vector.quantize_mx(
-                out=coef_codes[:, c, :].bitcast(FP8X4),
-                scales=coef_scales[:, c, :],
-                in_=grouped_sb[c][:].rearrange("p g o t -> p (g o t)"),
+                out=coef_codes[:, c, cols].bitcast(FP8X4),
+                scales=coef_scales[:, c, cols],
+                in_=grouped_sb[c][:, gs].rearrange("p g o t -> p (g o t)"),
             )
 
         rwT_first = psum.tile([P, O_TILES // 2, P], BF16, tag=RW_BANK)
@@ -200,12 +205,11 @@ def tile_bsplinebasis_v2_s_kernel(
         def dist_view(g, bs):
             return dist[g][:, :, bs, :].rearrange("p e b u -> p (b u) e")
 
-        def distances(g):
-            for e in range(2):
-                nc.scalar.activation(
-                    out=dist[g][:, e], in_=u_ps[g][:].rearrange("p u b -> p b u"),
-                    func=ACT.Abs, scale=2.5, bias=centre[:, e : e + 1],
-                )
+        def distance(g, e):
+            nc.scalar.activation(
+                out=dist[g][:, e], in_=u_ps[g][:].rearrange("p u b -> p b u"),
+                func=ACT.Abs, scale=2.5, bias=centre[:, e : e + 1],
+            )
 
         def square(out, root, centre_at, g, bs):
             nc.scalar.activation(
@@ -233,11 +237,15 @@ def tile_bsplinebasis_v2_s_kernel(
             )
 
         first_half, second_half, both = slice(0, P // 2), slice(P // 2, P), slice(0, P)
-        distances(0)
+        distance(0, 0)
+        distance(0, 1)
+        distance(1, 0)
         square(wide_sq[0], root_sixth, 2.0, 0, first_half)
         square(wide_sq[0], root_sixth, 2.0, 0, second_half)
         square(narrow_sq[0], root_two_thirds, 1.0, 0, both)
-        distances(1)
+        distance(1, 1)
+        nc.scalar.copy(out=bias_col[:], in_=small_ps[:, 1, 0:O_PAIRS].bitcast(BF16))
+        nc.scalar.copy(out=rwT_sb[1][:], in_=rwT_ps[1])
         square(wide_sq[1], root_sixth, 2.0, 1, both)
         square(narrow_sq[1], root_two_thirds, 1.0, 1, both)
 
@@ -249,14 +257,12 @@ def tile_bsplinebasis_v2_s_kernel(
         cube(wide_cube[0], 2.0, 0, first_half, wide_sq[0])
         cube(wide_cube[0], 2.0, 0, second_half, wide_sq[0])
         cube(narrow_cube[0], 1.0, 0, both, narrow_sq[0])
-        nc.vector.tensor_copy(out=rwT_sb[1][:], in_=rwT_ps[1])
         combine(0)
         cube(wide_cube[1], 2.0, 1, both, wide_sq[1])
         cut(0)
         cube(narrow_cube[1], 1.0, 1, both, narrow_sq[1])
         quantise_basis(0)
         combine(1)
-        nc.scalar.copy(out=bias_col[:], in_=small_ps[:, 1, 0:O_PAIRS].bitcast(BF16))
 
         out_ps = {}
 
@@ -275,18 +281,40 @@ def tile_bsplinebasis_v2_s_kernel(
             transpose_tile(c)
         open_pair(0)
         open_pair(1)
-        for c in range(O_TILES):
+        for c in range(O_TILES - 1):
             regroup(c)
             if c + 6 < O_TILES:
                 transpose_tile(c + 6)
+        for g in range(PASSES):
+            regroup(O_TILES - 1, slice(g, g + 1))
         open_pair(2)
-        open_pair(3)
+        direct_ps = psum.tile([P, 4, P], F32, tag=OUT_BANKS[3])
+        direct_resid = direct_ps[:, 0:2, :].rearrange("b t p -> b (t p)")
+        nc.tensor.matmul(
+            out=direct_resid, lhsT=xT_sb[:],
+            rhs=rwT_sb[1][:, 2:4, :].rearrange("i c p -> i (c p)"), start=True, stop=False,
+        )
+        nc.tensor.matmul(
+            out=direct_resid, lhsT=ident_bf[:, O_PAIRS - 1 : O_PAIRS].to_broadcast([P, P]),
+            rhs=bias_rows[:], start=False, stop=True,
+        )
+        for n in range(2):
+            c = PAIRED + n
+            nc.tensor.transpose(
+                direct_ps[:, 2 + n, :], scale_col[:, c : c + 1].to_broadcast([P, P]), ident_f32[:]
+            )
         quantise_coef(0)
         cut(1)
         quantise_coef(1)
         quantise_basis(1)
-        for c in range(2, O_TILES):
+        for c in range(2, 5):
             quantise_coef(c)
+        scale_wide = stage.tile([P, 2, P], F32)
+        nc.vector.tensor_copy(out=scale_wide[:], in_=direct_ps[:, 2:4, :])
+        for c in range(5, O_TILES - 1):
+            quantise_coef(c)
+        for g in range(PASSES):
+            quantise_coef(O_TILES - 1, slice(g, g + 1))
 
         spline_ps = {}
         scaled_sb = {}
@@ -307,19 +335,27 @@ def tile_bsplinebasis_v2_s_kernel(
                     )
                 spline_ps[c] = spline[:, n, :]
 
-        def scale_tile(c, on_scalar):
+        def multiply_direct(c):
+            spline = psum.tile([P, P], F32, name="spline_direct", tag=SPLINE_BANKS[c])
+            for g in range(PASSES):
+                cols = slice(g * P, (g + 1) * P)
+                nc.tensor.matmul_mx(
+                    out=spline[:],
+                    lhsT=basis_codes[:, g, :].bitcast(FP8X4),
+                    lhsT_scale=basis_scales[:, g, :],
+                    rhs=coef_codes[:, c, cols].bitcast(FP8X4),
+                    rhs_scale=coef_scales[:, c, cols],
+                    start=(g == 0),
+                    stop=(g == PASSES - 1),
+                )
+            spline_ps[c] = spline[:]
+
+        def scale_tile(c):
             scaled = stage.tile([P, P], F32, name="scaled")
-            if on_scalar:
-                nc.scalar.activation(
-                    out=scaled[:], in_=spline_ps[c], func=ACT.Identity,
-                    scale=scale_col[:, c : c + 1], bias=bias_col[:, c : c + 1],
-                )
-            else:
-                nc.vector.tensor_scalar(
-                    out=scaled[:], in0=spline_ps[c],
-                    scalar1=scale_col[:, c : c + 1], scalar2=bias_col[:, c : c + 1],
-                    op0=ALU.mult, op1=ALU.add,
-                )
+            nc.scalar.activation(
+                out=scaled[:], in_=spline_ps[c], func=ACT.Identity,
+                scale=scale_col[:, c : c + 1], bias=bias_col[:, c : c + 1],
+            )
             scaled_sb[c] = scaled
 
         def add_pair(h):
@@ -339,14 +375,24 @@ def tile_bsplinebasis_v2_s_kernel(
 
         multiply((0, 1, 2, 3))
         multiply((4, 5))
-        multiply((6,))
-        multiply((7,))
-        for c in range(6):
-            scale_tile(c, True)
-        for c in (6, 7):
-            scale_tile(c, False)
-        for h in range(O_PAIRS):
-            add_pair(h)
-        for h in range(O_PAIRS - 1):
+        for c in range(PAIRED):
+            scale_tile(c)
+        multiply_direct(6)
+        add_pair(0)
+        multiply_direct(7)
+        add_pair(1)
+        add_pair(2)
+        store_pair(0, nc.vector.tensor_copy)
+        product = stage.tile([P, 2, P], F32)
+        direct_sb = stage.tile([P, 2, P], F32)
+        for n in range(2):
+            nc.vector.tensor_mul(
+                out=product[:, n, :], in0=spline_ps[PAIRED + n], in1=scale_wide[:, n, :]
+            )
+        for n in range(2):
+            nc.vector.tensor_add(
+                out=direct_sb[:, n, :], in0=direct_ps[:, n, :], in1=product[:, n, :]
+            )
+        for h in range(1, PAIRED // 2):
             store_pair(h, nc.scalar.copy)
-        store_pair(O_PAIRS - 1, nc.vector.tensor_copy)
+        nc.sync.dma_start(out=out[:, PAIRED * P :], in_=direct_sb[:].rearrange("b t p -> b (t p)"))

@@ -47,12 +47,8 @@ def tile_bsplinebasis_v2_s_kernel(
 
         def load_rows(tile, rows):
             nc.sync.dma_start(
-                out=tile[:, :PAIRED, :].rearrange("p (h t) i -> p h (t i)", t=2),
-                in_=rows[: PAIRED * P].rearrange("(h p t) i -> p h (t i)", p=P, t=2),
-            )
-            nc.sync.dma_start(
-                out=tile[:, PAIRED:, :],
-                in_=rows[PAIRED * P :].rearrange("(t p) i -> p t i", p=P),
+                out=tile[:].rearrange("p (h t) i -> p h (t i)", t=2),
+                in_=rows.rearrange("(h p t) i -> p h (t i)", p=P, t=2),
             )
 
         x_sb = keep.tile([P, P], BF16)
@@ -70,10 +66,11 @@ def tile_bsplinebasis_v2_s_kernel(
         coef_sb = []
         for h in range(O_PAIRS):
             coef_h = coef_pool.tile([P, 2, K], BF16, name="coef_h")
-            order = "(p t) i j -> p t (i j)" if 2 * h < PAIRED else "(t p) i j -> p t (i j)"
             nc.sync.dma_start(
                 out=coef_h[:],
-                in_=spline_coeffs[2 * h * P : 2 * (h + 1) * P].rearrange(order, t=2),
+                in_=spline_coeffs[2 * h * P : 2 * (h + 1) * P].rearrange(
+                    "(p t) i j -> p t (i j)", t=2
+                ),
             )
             coef_sb.append(coef_h)
 
@@ -192,18 +189,15 @@ def tile_bsplinebasis_v2_s_kernel(
         dist, wide_sq, narrow_sq, wide_cube, narrow_cube, uncut = [], [], [], [], [], []
         for g in range(PASSES):
             dist.append(work.tile([P, 2, P, 2], F32, name="dist"))
-            wide_sq.append(work.tile([P, P, 2, 2], F32, name="wide_sq"))
-            narrow_sq.append(work.tile([P, P, 2, 2], F32, name="narrow_sq"))
-            wide_cube.append(work.tile([P, P, 2, 2], F32, name="wide_cube"))
-            narrow_cube.append(work.tile([P, P, 2, 2], F32, name="narrow_cube"))
+            wide_sq.append(work.tile([P, 2, P, 2], F32, name="wide_sq"))
+            narrow_sq.append(work.tile([P, 2, P, 2], F32, name="narrow_sq"))
+            wide_cube.append(work.tile([P, 2, P, 2], F32, name="wide_cube"))
+            narrow_cube.append(work.tile([P, 2, P, 2], F32, name="narrow_cube"))
             uncut.append(work.tile([P, P, 2, 2], BF16, name="uncut"))
             basis_bf.append(work.tile([P, P, 2, 2], BF16, align_bytes=64, name="basis_g"))
 
-        def flat(ap):
-            return ap.rearrange("p b u e -> p (b u) e")
-
-        def dist_view(g, bs):
-            return dist[g][:, :, bs, :].rearrange("p e b u -> p (b u) e")
+        def flat(tile, es):
+            return tile[:, es].rearrange("p e b u -> p (e b u)")
 
         def distance(g, e):
             nc.scalar.activation(
@@ -211,22 +205,23 @@ def tile_bsplinebasis_v2_s_kernel(
                 func=ACT.Abs, scale=2.5, bias=centre[:, e : e + 1],
             )
 
-        def square(out, root, centre_at, g, bs):
+        def square(out, root, centre_at, g, es):
             nc.scalar.activation(
-                out=flat(out[:, bs]), in_=dist_view(g, bs), func=ACT.Square,
+                out=flat(out, es), in_=flat(dist[g], es), func=ACT.Square,
                 scale=root, bias=-centre_at * root,
             )
 
-        def cube(out, centre_at, g, bs, sq):
+        def cube(out, centre_at, g, es, sq):
             nc.vector.scalar_tensor_tensor(
-                out=flat(out[:, bs]), in0=dist_view(g, bs),
-                scalar=centre_at, in1=flat(sq[:, bs]), op0=ALU.subtract, op1=ALU.mult,
+                out=flat(out, es), in0=flat(dist[g], es),
+                scalar=centre_at, in1=flat(sq, es), op0=ALU.subtract, op1=ALU.mult,
             )
 
         def combine(g):
             nc.vector.scalar_tensor_tensor(
-                out=flat(uncut[g][:]), in0=flat(narrow_cube[g][:]),
-                scalar=0.0, in1=flat(wide_cube[g][:]),
+                out=uncut[g][:].rearrange("p b u e -> p (b u) e"),
+                in0=narrow_cube[g][:].rearrange("p e b u -> p (b u) e"),
+                scalar=0.0, in1=wide_cube[g][:].rearrange("p e b u -> p (b u) e"),
                 op0=ALU.min, op1=ALU.subtract,
             )
 
@@ -236,17 +231,16 @@ def tile_bsplinebasis_v2_s_kernel(
                 in0=uncut[g][:].rearrange("p b u e -> p (b u e)"), scalar1=0.0,
             )
 
-        first_half, second_half, both = slice(0, P // 2), slice(P // 2, P), slice(0, P)
+        first, second, both = slice(0, 1), slice(1, 2), slice(0, 2)
         distance(0, 0)
         distance(0, 1)
-        distance(1, 0)
-        square(wide_sq[0], root_sixth, 2.0, 0, first_half)
-        square(wide_sq[0], root_sixth, 2.0, 0, second_half)
+        square(wide_sq[0], root_sixth, 2.0, 0, first)
+        square(wide_sq[0], root_sixth, 2.0, 0, second)
         square(narrow_sq[0], root_two_thirds, 1.0, 0, both)
+        distance(1, 0)
         distance(1, 1)
-        nc.scalar.copy(out=bias_col[:], in_=small_ps[:, 1, 0:O_PAIRS].bitcast(BF16))
-        nc.scalar.copy(out=rwT_sb[1][:], in_=rwT_ps[1])
-        square(wide_sq[1], root_sixth, 2.0, 1, both)
+        square(wide_sq[1], root_sixth, 2.0, 1, first)
+        square(wide_sq[1], root_sixth, 2.0, 1, second)
         square(narrow_sq[1], root_two_thirds, 1.0, 1, both)
 
         nc.gpsimd.tensor_scalar(
@@ -254,8 +248,9 @@ def tile_bsplinebasis_v2_s_kernel(
             op0=ALU.mult, op1=ALU.add,
         )
         nc.vector.tensor_copy(out=rwT_sb[0][:], in_=rwT_ps[0])
-        cube(wide_cube[0], 2.0, 0, first_half, wide_sq[0])
-        cube(wide_cube[0], 2.0, 0, second_half, wide_sq[0])
+        cube(wide_cube[0], 2.0, 0, first, wide_sq[0])
+        cube(wide_cube[0], 2.0, 0, second, wide_sq[0])
+        nc.vector.tensor_copy(out=rwT_sb[1][:], in_=rwT_ps[1])
         cube(narrow_cube[0], 1.0, 0, both, narrow_sq[0])
         combine(0)
         cube(wide_cube[1], 2.0, 1, both, wide_sq[1])
@@ -263,6 +258,7 @@ def tile_bsplinebasis_v2_s_kernel(
         cube(narrow_cube[1], 1.0, 1, both, narrow_sq[1])
         quantise_basis(0)
         combine(1)
+        nc.scalar.copy(out=bias_col[:], in_=small_ps[:, 1, 0:O_PAIRS].bitcast(BF16))
 
         out_ps = {}
 
@@ -289,14 +285,14 @@ def tile_bsplinebasis_v2_s_kernel(
             regroup(O_TILES - 1, slice(g, g + 1))
         open_pair(2)
         direct_ps = psum.tile([P, 4, P], F32, tag=OUT_BANKS[3])
-        direct_resid = direct_ps[:, 0:2, :].rearrange("b t p -> b (t p)")
+        direct_resid = direct_ps[:, 0:2, :]
         nc.tensor.matmul(
             out=direct_resid, lhsT=xT_sb[:],
-            rhs=rwT_sb[1][:, 2:4, :].rearrange("i c p -> i (c p)"), start=True, stop=False,
+            rhs=rwT_sb[1][:, 2:4, :], start=True, stop=False,
         )
         nc.tensor.matmul(
             out=direct_resid, lhsT=ident_bf[:, O_PAIRS - 1 : O_PAIRS].to_broadcast([P, P]),
-            rhs=bias_rows[:], start=False, stop=True,
+            rhs=bias_rows[:].rearrange("k (p t) -> k t p", t=2), start=False, stop=True,
         )
         for n in range(2):
             c = PAIRED + n
@@ -307,11 +303,7 @@ def tile_bsplinebasis_v2_s_kernel(
         cut(1)
         quantise_coef(1)
         quantise_basis(1)
-        for c in range(2, 5):
-            quantise_coef(c)
-        scale_wide = stage.tile([P, 2, P], F32)
-        nc.vector.tensor_copy(out=scale_wide[:], in_=direct_ps[:, 2:4, :])
-        for c in range(5, O_TILES - 1):
+        for c in range(2, O_TILES - 1):
             quantise_coef(c)
         for g in range(PASSES):
             quantise_coef(O_TILES - 1, slice(g, g + 1))
@@ -382,17 +374,18 @@ def tile_bsplinebasis_v2_s_kernel(
         multiply_direct(7)
         add_pair(1)
         add_pair(2)
-        store_pair(0, nc.vector.tensor_copy)
+        scale_wide = stage.tile([P, 2, P], F32)
+        nc.vector.tensor_copy(out=scale_wide[:], in_=direct_ps[:, 2:4, :])
         product = stage.tile([P, 2, P], F32)
-        direct_sb = stage.tile([P, 2, P], F32)
         for n in range(2):
             nc.vector.tensor_mul(
                 out=product[:, n, :], in0=spline_ps[PAIRED + n], in1=scale_wide[:, n, :]
             )
-        for n in range(2):
-            nc.vector.tensor_add(
-                out=direct_sb[:, n, :], in0=direct_ps[:, n, :], in1=product[:, n, :]
-            )
-        for h in range(1, PAIRED // 2):
+        direct_sb = stage.tile([P, P, 2], F32)
+        nc.vector.tensor_add(
+            out=direct_sb[:], in0=direct_ps[:, 0:2, :].rearrange("b t p -> b p t"),
+            in1=product[:].rearrange("b t p -> b p t"),
+        )
+        for h in range(PAIRED // 2):
             store_pair(h, nc.scalar.copy)
-        nc.sync.dma_start(out=out[:, PAIRED * P :], in_=direct_sb[:].rearrange("b t p -> b (t p)"))
+        nc.sync.dma_start(out=out[:, PAIRED * P :], in_=direct_sb[:].rearrange("b p t -> b (p t)"))

@@ -250,8 +250,8 @@ def tile_bsplinebasis_v2_s_kernel(
         nc.vector.tensor_copy(out=rwT_sb[0][:], in_=rwT_ps[0])
         cube(wide_cube[0], 2.0, 0, first, wide_sq[0])
         cube(wide_cube[0], 2.0, 0, second, wide_sq[0])
-        nc.vector.tensor_copy(out=rwT_sb[1][:], in_=rwT_ps[1])
         cube(narrow_cube[0], 1.0, 0, both, narrow_sq[0])
+        nc.vector.tensor_copy(out=rwT_sb[1][:], in_=rwT_ps[1])
         combine(0)
         cube(wide_cube[1], 2.0, 1, both, wide_sq[1])
         cut(0)
@@ -367,6 +367,8 @@ def tile_bsplinebasis_v2_s_kernel(
 
         multiply((0, 1, 2, 3))
         multiply((4, 5))
+        scale_wide = stage.tile([P, 2, P], F32)
+        nc.scalar.copy(out=scale_wide[:], in_=direct_ps[:, 2:4, :])
         for c in range(PAIRED):
             scale_tile(c)
         multiply_direct(6)
@@ -374,18 +376,17 @@ def tile_bsplinebasis_v2_s_kernel(
         multiply_direct(7)
         add_pair(1)
         add_pair(2)
-        scale_wide = stage.tile([P, 2, P], F32)
-        nc.vector.tensor_copy(out=scale_wide[:], in_=direct_ps[:, 2:4, :])
         product = stage.tile([P, 2, P], F32)
         for n in range(2):
             nc.vector.tensor_mul(
                 out=product[:, n, :], in0=spline_ps[PAIRED + n], in1=scale_wide[:, n, :]
             )
+        store_pair(0, nc.vector.tensor_copy)
         direct_sb = stage.tile([P, P, 2], F32)
         nc.vector.tensor_add(
             out=direct_sb[:], in0=direct_ps[:, 0:2, :].rearrange("b t p -> b p t"),
             in1=product[:].rearrange("b t p -> b p t"),
         )
-        for h in range(PAIRED // 2):
+        for h in range(1, PAIRED // 2):
             store_pair(h, nc.scalar.copy)
         nc.sync.dma_start(out=out[:, PAIRED * P :], in_=direct_sb[:].rearrange("b p t -> b (p t)"))

@@ -43,7 +43,7 @@ def tile_bsplinebasis_v2_s_kernel(
         SMALL_BANK, RW_BANK = "b2", "b3"
         COEF_BANKS = ("b4", "b5", "b6", "b7", "b0", "b1", "b4", "b5")
         OUT_BANKS = ("b3", "b2", "b6", "b7")
-        SPLINE_BANKS = ("b0", "b0", "b0", "b0", "b1", "b1", "b4", "b5")
+        SPLINE_BANKS = ("b0", "b0", "b1", "b1", "b4", "b4", "b5", "b5")
 
         def load_rows(tile, rows):
             nc.sync.dma_start(
@@ -275,15 +275,10 @@ def tile_bsplinebasis_v2_s_kernel(
 
         for c in range(6):
             transpose_tile(c)
-        open_pair(0)
-        open_pair(1)
-        for c in range(O_TILES - 1):
+        for c in range(4):
             regroup(c)
-            if c + 6 < O_TILES:
-                transpose_tile(c + 6)
-        for g in range(PASSES):
-            regroup(O_TILES - 1, slice(g, g + 1))
-        open_pair(2)
+        for h in range(PAIRED // 2):
+            open_pair(h)
         direct_ps = psum.tile([P, 4, P], F32, tag=OUT_BANKS[3])
         direct_resid = direct_ps[:, 0:2, :]
         nc.tensor.matmul(
@@ -299,6 +294,12 @@ def tile_bsplinebasis_v2_s_kernel(
             nc.tensor.transpose(
                 direct_ps[:, 2 + n, :], scale_col[:, c : c + 1].to_broadcast([P, P]), ident_f32[:]
             )
+        for c in range(4, O_TILES - 1):
+            regroup(c)
+            if c < 6:
+                transpose_tile(c + 2)
+        for g in range(PASSES):
+            regroup(O_TILES - 1, slice(g, g + 1))
         quantise_coef(0)
         cut(1)
         quantise_coef(1)
@@ -327,20 +328,21 @@ def tile_bsplinebasis_v2_s_kernel(
                     )
                 spline_ps[c] = spline[:, n, :]
 
-        def multiply_direct(c):
-            spline = psum.tile([P, P], F32, name="spline_direct", tag=SPLINE_BANKS[c])
-            for g in range(PASSES):
-                cols = slice(g * P, (g + 1) * P)
-                nc.tensor.matmul_mx(
-                    out=spline[:],
-                    lhsT=basis_codes[:, g, :].bitcast(FP8X4),
-                    lhsT_scale=basis_scales[:, g, :],
-                    rhs=coef_codes[:, c, cols].bitcast(FP8X4),
-                    rhs_scale=coef_scales[:, c, cols],
-                    start=(g == 0),
-                    stop=(g == PASSES - 1),
-                )
-            spline_ps[c] = spline[:]
+        def multiply_direct():
+            spline = psum.tile([P, 2, P], F32, name="spline_direct", tag=SPLINE_BANKS[PAIRED])
+            for n in range(2):
+                for g in range(PASSES):
+                    cols = slice(g * P, (g + 1) * P)
+                    nc.tensor.matmul_mx(
+                        out=spline[:, n, :],
+                        lhsT=basis_codes[:, g, :].bitcast(FP8X4),
+                        lhsT_scale=basis_scales[:, g, :],
+                        rhs=coef_codes[:, PAIRED + n, cols].bitcast(FP8X4),
+                        rhs_scale=coef_scales[:, PAIRED + n, cols],
+                        start=(g == 0),
+                        stop=(g == PASSES - 1),
+                    )
+            return spline
 
         def scale_tile(c):
             scaled = stage.tile([P, P], F32, name="scaled")
@@ -365,28 +367,23 @@ def tile_bsplinebasis_v2_s_kernel(
                 in_=out_sb[:].rearrange("b p t -> b (p t)"),
             )
 
-        multiply((0, 1, 2, 3))
-        multiply((4, 5))
-        scale_wide = stage.tile([P, 2, P], F32)
-        nc.scalar.copy(out=scale_wide[:], in_=direct_ps[:, 2:4, :])
+        for h in range(PAIRED // 2):
+            multiply((2 * h, 2 * h + 1))
+        direct_spline = multiply_direct()
         for c in range(PAIRED):
             scale_tile(c)
-        multiply_direct(6)
-        add_pair(0)
-        multiply_direct(7)
-        add_pair(1)
-        add_pair(2)
+        for h in range(PAIRED // 2):
+            add_pair(h)
+        scale_wide = stage.tile([P, 2, P], F32)
+        nc.vector.tensor_copy(out=scale_wide[:], in_=direct_ps[:, 2:4, :])
         product = stage.tile([P, 2, P], F32)
-        for n in range(2):
-            nc.vector.tensor_mul(
-                out=product[:, n, :], in0=spline_ps[PAIRED + n], in1=scale_wide[:, n, :]
-            )
-        store_pair(0, nc.vector.tensor_copy)
+        nc.vector.tensor_mul(out=product[:], in0=direct_spline[:], in1=scale_wide[:])
+        store_pair(0, nc.scalar.copy)
+        store_pair(1, nc.vector.tensor_copy)
         direct_sb = stage.tile([P, P, 2], F32)
         nc.vector.tensor_add(
             out=direct_sb[:], in0=direct_ps[:, 0:2, :].rearrange("b t p -> b p t"),
             in1=product[:].rearrange("b t p -> b p t"),
         )
-        for h in range(1, PAIRED // 2):
-            store_pair(h, nc.scalar.copy)
+        store_pair(2, nc.scalar.copy)
         nc.sync.dma_start(out=out[:, PAIRED * P :], in_=direct_sb[:].rearrange("b p t -> b (p t)"))

@@ -41,9 +41,9 @@ def tile_bsplinebasis_v2_s_kernel(
         psum = ctx.enter_context(tc.psum_pool(name="psum", bufs=1))
         U_BANKS = ("b0", "b1")
         SMALL_BANK, RW_BANK = "b2", "b3"
-        COEF_BANKS = ("b4", "b5", "b6", "b7", "b0", "b1", "b4", "b5")
-        OUT_BANKS = ("b3", "b2", "b6", "b7")
-        SPLINE_BANKS = ("b0", "b0", "b1", "b1", "b4", "b4", "b5", "b5")
+        COEF_BANKS = ("b4", "b5", "b6", "b7", "b0", "b1", "b6", "b7")
+        OUT_BANKS = ("b3", "b2", "b4", "b5")
+        SPLINE_BANKS = ("b0", "b0", "b1", "b1", "b6", "b6", "b7", "b7")
 
         def load_rows(tile, rows):
             nc.sync.dma_start(
@@ -275,31 +275,30 @@ def tile_bsplinebasis_v2_s_kernel(
 
         for c in range(6):
             transpose_tile(c)
-        for c in range(4):
+        for c in range(2):
             regroup(c)
         for h in range(PAIRED // 2):
             open_pair(h)
         direct_ps = psum.tile([P, 4, P], F32, tag=OUT_BANKS[3])
-        direct_resid = direct_ps[:, 0:2, :]
         nc.tensor.matmul(
-            out=direct_resid, lhsT=xT_sb[:],
+            out=direct_ps[:, 0:2, :], lhsT=xT_sb[:],
             rhs=rwT_sb[1][:, 2:4, :], start=True, stop=False,
         )
         nc.tensor.matmul(
-            out=direct_resid, lhsT=ident_bf[:, O_PAIRS - 1 : O_PAIRS].to_broadcast([P, P]),
+            out=direct_ps[:, 0:2, :], lhsT=ident_bf[:, O_PAIRS - 1 : O_PAIRS].to_broadcast([P, P]),
             rhs=bias_rows[:].rearrange("k (p t) -> k t p", t=2), start=False, stop=True,
         )
+        for c in range(2, O_TILES - 1):
+            regroup(c)
+            if c < 4:
+                transpose_tile(c + 4)
+        for g in range(PASSES):
+            regroup(O_TILES - 1, slice(g, g + 1))
         for n in range(2):
             c = PAIRED + n
             nc.tensor.transpose(
                 direct_ps[:, 2 + n, :], scale_col[:, c : c + 1].to_broadcast([P, P]), ident_f32[:]
             )
-        for c in range(4, O_TILES - 1):
-            regroup(c)
-            if c < 6:
-                transpose_tile(c + 2)
-        for g in range(PASSES):
-            regroup(O_TILES - 1, slice(g, g + 1))
         quantise_coef(0)
         cut(1)
         quantise_coef(1)

@@ -171,12 +171,11 @@ def tile_bsplinebasis_v2_s_kernel(
         nc.tensor.transpose(small_ps[:, 1, :], bias_rows[:].bitcast(F32), ident_f32[:])
         rwT_sb = [keep.tile([P, O_TILES // 2, P], BF16, name="rwT_half%d" % n) for n in range(2)]
         bias_col = keep.tile([P, O_TILES], F32)
-        scale_col = keep.tile([P, O_TILES], F32)
 
         basis_codes = keep.tile([P, PASSES, P], U32, align_bytes=64)
         basis_scales = keep.tile([P, PASSES, P], U8, align_bytes=64)
-        root_sixth = 1.0 / math.sqrt(6.0)
-        root_two_thirds = math.sqrt(2.0 / 3.0)
+        root_sixth = 1.0 / math.sqrt(6.0 * P)
+        root_two_thirds = math.sqrt(2.0 / (3.0 * P))
         basis_bf = []
 
         def quantise_basis(g):
@@ -243,13 +242,9 @@ def tile_bsplinebasis_v2_s_kernel(
         square(wide_sq[1], root_sixth, 2.0, 1, second)
         square(narrow_sq[1], root_two_thirds, 1.0, 1, both)
 
-        nc.gpsimd.tensor_scalar(
-            out=scale_col[:], in0=base_sum[:], scalar1=1.0 / P, scalar2=0.0,
-            op0=ALU.mult, op1=ALU.add,
-        )
-        nc.vector.tensor_copy(out=rwT_sb[0][:], in_=rwT_ps[0])
         cube(wide_cube[0], 2.0, 0, first, wide_sq[0])
         cube(wide_cube[0], 2.0, 0, second, wide_sq[0])
+        nc.vector.tensor_copy(out=rwT_sb[0][:], in_=rwT_ps[0])
         cube(narrow_cube[0], 1.0, 0, both, narrow_sq[0])
         nc.vector.tensor_copy(out=rwT_sb[1][:], in_=rwT_ps[1])
         combine(0)
@@ -275,10 +270,15 @@ def tile_bsplinebasis_v2_s_kernel(
 
         for c in range(6):
             transpose_tile(c)
-        for c in range(2):
+        open_pair(0)
+        open_pair(1)
+        for c in range(O_TILES - 1):
             regroup(c)
-        for h in range(PAIRED // 2):
-            open_pair(h)
+            if c in (2, 3):
+                transpose_tile(c + 4)
+        for g in range(PASSES):
+            regroup(O_TILES - 1, slice(g, g + 1))
+        open_pair(2)
         direct_ps = psum.tile([P, 4, P], F32, tag=OUT_BANKS[3])
         nc.tensor.matmul(
             out=direct_ps[:, 0:2, :], lhsT=xT_sb[:],
@@ -288,16 +288,10 @@ def tile_bsplinebasis_v2_s_kernel(
             out=direct_ps[:, 0:2, :], lhsT=ident_bf[:, O_PAIRS - 1 : O_PAIRS].to_broadcast([P, P]),
             rhs=bias_rows[:].rearrange("k (p t) -> k t p", t=2), start=False, stop=True,
         )
-        for c in range(2, O_TILES - 1):
-            regroup(c)
-            if c < 4:
-                transpose_tile(c + 4)
-        for g in range(PASSES):
-            regroup(O_TILES - 1, slice(g, g + 1))
         for n in range(2):
             c = PAIRED + n
             nc.tensor.transpose(
-                direct_ps[:, 2 + n, :], scale_col[:, c : c + 1].to_broadcast([P, P]), ident_f32[:]
+                direct_ps[:, 2 + n, :], base_sum[:, c : c + 1].to_broadcast([P, P]), ident_f32[:]
             )
         quantise_coef(0)
         cut(1)
@@ -347,7 +341,7 @@ def tile_bsplinebasis_v2_s_kernel(
             scaled = stage.tile([P, P], F32, name="scaled")
             nc.scalar.activation(
                 out=scaled[:], in_=spline_ps[c], func=ACT.Identity,
-                scale=scale_col[:, c : c + 1], bias=bias_col[:, c : c + 1],
+                scale=base_sum[:, c : c + 1], bias=bias_col[:, c : c + 1],
             )
             scaled_sb[c] = scaled
 

@@ -278,16 +278,7 @@ def tile_bsplinebasis_v2_s_kernel(
                 transpose_tile(c + 4)
         for g in range(PASSES):
             regroup(O_TILES - 1, slice(g, g + 1))
-        open_pair(2)
         direct_ps = psum.tile([P, 4, P], F32, tag=OUT_BANKS[3])
-        nc.tensor.matmul(
-            out=direct_ps[:, 0:2, :], lhsT=xT_sb[:],
-            rhs=rwT_sb[1][:, 2:4, :], start=True, stop=False,
-        )
-        nc.tensor.matmul(
-            out=direct_ps[:, 0:2, :], lhsT=ident_bf[:, O_PAIRS - 1 : O_PAIRS].to_broadcast([P, P]),
-            rhs=bias_rows[:].rearrange("k (p t) -> k t p", t=2), start=False, stop=True,
-        )
         for n in range(2):
             c = PAIRED + n
             nc.tensor.transpose(
@@ -360,19 +351,30 @@ def tile_bsplinebasis_v2_s_kernel(
                 in_=out_sb[:].rearrange("b p t -> b (p t)"),
             )
 
-        for h in range(PAIRED // 2):
-            multiply((2 * h, 2 * h + 1))
-        direct_spline = multiply_direct()
+        multiply((0, 1))
+        multiply((2, 3))
+        open_pair(2)
+        nc.tensor.matmul(
+            out=direct_ps[:, 0:2, :], lhsT=xT_sb[:],
+            rhs=rwT_sb[1][:, 2:4, :], start=True, stop=False,
+        )
+        nc.tensor.matmul(
+            out=direct_ps[:, 0:2, :], lhsT=ident_bf[:, O_PAIRS - 1 : O_PAIRS].to_broadcast([P, P]),
+            rhs=bias_rows[:].rearrange("k (p t) -> k t p", t=2), start=False, stop=True,
+        )
+        multiply((4, 5))
         for c in range(PAIRED):
             scale_tile(c)
-        for h in range(PAIRED // 2):
+        add_pair(0)
+        direct_spline = multiply_direct()
+        for h in range(1, PAIRED // 2):
             add_pair(h)
         scale_wide = stage.tile([P, 2, P], F32)
         nc.vector.tensor_copy(out=scale_wide[:], in_=direct_ps[:, 2:4, :])
         product = stage.tile([P, 2, P], F32)
         nc.vector.tensor_mul(out=product[:], in0=direct_spline[:], in1=scale_wide[:])
         store_pair(0, nc.scalar.copy)
-        store_pair(1, nc.vector.tensor_copy)
+        store_pair(1, nc.scalar.copy)
         direct_sb = stage.tile([P, P, 2], F32)
         nc.vector.tensor_add(
             out=direct_sb[:], in0=direct_ps[:, 0:2, :].rearrange("b t p -> b p t"),

from contextlib import ExitStack
import math

import concourse.mybir as mybir
from concourse.masks import make_identity

F32 = mybir.dt.float32
BF16 = mybir.dt.bfloat16
I32 = mybir.dt.int32
U32 = mybir.dt.uint32
U8 = mybir.dt.uint8
FP8X4 = mybir.dt.float8_e4m3fn_x4
ALU = mybir.AluOpType
ACT = mybir.ActivationFunctionType
AX = mybir.AxisListType

P = 128
NB = 8
K = P * NB
O = 1024
O_TILES = O // P
O_PAIRS = O_TILES // 2
PASSES = 2
PAIRED = 6

FLOPS = 2 * P * K * O + 2 * P * P * O


def tile_bsplinebasis_v2_s_kernel(
    tc, x, spline_coeffs, residual_weight, residual_bias, scale_base, out
):
    nc = tc.nc
    with ExitStack() as ctx:
        ctx.enter_context(tc.manual_schedule())
        const = ctx.enter_context(tc.tile_pool(name="const", bufs=1))
        keep = ctx.enter_context(tc.tile_pool(name="keep", bufs=1))
        work = ctx.enter_context(tc.tile_pool(name="work", bufs=2))
        coef_pool = ctx.enter_context(tc.tile_pool(name="coef", bufs=O_PAIRS))
        group_pool = ctx.enter_context(tc.tile_pool(name="group", bufs=O_TILES))
        stage = ctx.enter_context(tc.tile_pool(name="stage", bufs=O_TILES))
        psum = ctx.enter_context(tc.psum_pool(name="psum", bufs=1))
        U_BANKS = ("b0", "b1")
        SMALL_BANK, RW_BANK = "b2", "b3"
        COEF_BANKS = ("b4", "b5", "b6", "b7", "b0", "b1", "b6", "b7")
        OUT_BANKS = ("b3", "b2", "b4", "b5")
        SPLINE_BANKS = ("b0", "b0", "b1", "b1", "b6", "b6", "b7", "b7")

        def load_rows(tile, rows):
            nc.sync.dma_start(
                out=tile[:].rearrange("p (h t) i -> p h (t i)", t=2),
                in_=rows.rearrange("(h p t) i -> p h (t i)", p=P, t=2),
            )

        x_sb = keep.tile([P, P], BF16)
        nc.sync.dma_start(out=x_sb[:], in_=x)
        bias_rows = keep.tile([P, 2 * P], BF16)
        nc.vector.memset(bias_rows[:], 0.0)
        base_sb = keep.tile([P, O_TILES, P], BF16)
        load_rows(base_sb, scale_base)
        rw_sb = keep.tile([P, O_TILES, P], BF16)
        load_rows(rw_sb, residual_weight)
        nc.sync.dma_start(
            out=bias_rows[0:O_PAIRS, :],
            in_=residual_bias.rearrange("(h n) -> h n", h=O_PAIRS),
        )
        coef_sb = []
        for h in range(O_PAIRS):
            coef_h = coef_pool.tile([P, 2, K], BF16, name="coef_h")
            nc.sync.dma_start(
                out=coef_h[:],
                in_=spline_coeffs[2 * h * P : 2 * (h + 1) * P].rearrange(
                    "(p t) i j -> p t (i j)", t=2
                ),
            )
            coef_sb.append(coef_h)

        zero_col = const.tile([P, 1], F32)
        nc.vector.memset(zero_col[:], 0.0)
        warm = const.tile([P, 1], F32)
        nc.scalar.activation(out=warm[:], in_=zero_col[:], func=ACT.Abs)
        ident_f32 = const.tile([P, P], F32)
        make_identity(nc, ident_f32[:])
        ident_bf = const.tile([P, P], BF16)
        nc.vector.tensor_copy(out=ident_bf[:], in_=ident_f32[:])
        part_index = const.tile([P, 1], I32)
        nc.gpsimd.iota(part_index[:], pattern=[[0, 1]], base=0, channel_multiplier=1)
        part_mod4 = const.tile([P, 1], I32)
        nc.vector.tensor_single_scalar(
            out=part_mod4[:], in_=part_index[:], scalar=3, op=ALU.bitwise_and
        )
        part_mod4_f = const.tile([P, 1], F32)
        nc.vector.tensor_copy(out=part_mod4_f[:], in_=part_mod4[:])
        centre = const.tile([P, 2], F32)
        for e in range(2):
            nc.vector.tensor_scalar(
                out=centre[:, e : e + 1],
                in0=part_mod4_f[:],
                scalar1=-2.0,
                scalar2=3.5 - e,
                op0=ALU.mult,
                op1=ALU.add,
            )

        half = P // PASSES
        small_ps = psum.tile([P, 4, P], F32, tag=SMALL_BANK)
        xT_ps = small_ps[:, 0, 0 : P // 2].bitcast(BF16)
        nc.tensor.transpose(xT_ps, x_sb[:], ident_bf[:])
        xT_sb = keep.tile([P, P], BF16)
        nc.scalar.copy(out=xT_sb[:], in_=xT_ps)
        clamped = keep.tile([P, P, 4], BF16)
        u_ps = []
        for g in range(PASSES):
            feats = slice(g * half, (g + 1) * half)
            nc.vector.tensor_scalar(
                out=clamped[:, feats, :],
                in0=x_sb[:, feats].unsqueeze(2).to_broadcast([P, half, 4]),
                scalar1=-1.0,
                scalar2=1.0,
                op0=ALU.max,
                op1=ALU.min,
            )
            u_g = psum.tile([P, 2, P], BF16, name="u_g", tag=U_BANKS[g])
            for u in range(2):
                first = g * half + u * (half // 2)
                nc.tensor.transpose(
                    u_g[:, u, :],
                    clamped[:, first : first + half // 2, :].rearrange("b i r -> b (i r)"),
                    ident_bf[:],
                )
            u_ps.append(u_g)

        base_sum = keep.tile([P, O_TILES], F32)
        nc.vector.tensor_reduce(out=base_sum[:], in_=base_sb[:], axis=AX.X, op=ALU.add)

        coef_codes = keep.tile([P, O_TILES, PASSES * P], U32, align_bytes=64)
        coef_scales = keep.tile([P, O_TILES, PASSES * P], U8, align_bytes=64)
        words_ps = {}

        def transpose_tile(c):
            coef_words = coef_sb[c // 2][:, c % 2, :].bitcast(F32)
            words_c = psum.tile([P, 2 * PASSES, P], F32, name="words_c", tag=COEF_BANKS[c])
            for m in range(2 * PASSES):
                nc.tensor.transpose(
                    words_c[:, m, :], coef_words[:, m * P : (m + 1) * P], ident_f32[:]
                )
            words_ps[c] = words_c

        grouped_sb = {}
        whole = slice(0, PASSES)

        def regroup(c, gs=whole):
            if c not in grouped_sb:
                grouped_sb[c] = group_pool.tile([P, PASSES, P, 4], BF16, align_bytes=64, name="grouped")
            nc.scalar.copy(
                out=grouped_sb[c][:, gs].bitcast(F32),
                in_=words_ps[c][:, 2 * gs.start : 2 * gs.stop].rearrange("p (g u) o -> p g o u", u=2),
            )

        def quantise_coef(c, gs=whole):
            cols = slice(gs.start * P, gs.stop * P)
            nc.vector.quantize_mx(
                out=coef_codes[:, c, cols].bitcast(FP8X4),
                scales=coef_scales[:, c, cols],
                in_=grouped_sb[c][:, gs].rearrange("p g o t -> p (g o t)"),
            )

        rwT_first = psum.tile([P, O_TILES // 2, P], BF16, tag=RW_BANK)
        rwT_ps = [rwT_first[:], small_ps[:, 2:4, :].bitcast(BF16).rearrange("i w (c p) -> i (w c) p", p=P)]
        for c in range(O_TILES):
            nc.tensor.transpose(rwT_ps[c // 4][:, c % 4, :], rw_sb[:, c, :], ident_bf[:])
        nc.tensor.transpose(small_ps[:, 1, :], bias_rows[:].bitcast(F32), ident_f32[:])
        rwT_sb = [keep.tile([P, O_TILES // 2, P], BF16, name="rwT_half%d" % n) for n in range(2)]
        bias_col = keep.tile([P, O_TILES], F32)

        basis_codes = keep.tile([P, PASSES, P], U32, align_bytes=64)
        basis_scales = keep.tile([P, PASSES, P], U8, align_bytes=64)
        root_sixth = 1.0 / math.sqrt(6.0 * P)
        root_two_thirds = math.sqrt(2.0 / (3.0 * P))
        basis_bf = []

        def quantise_basis(g):
            nc.vector.quantize_mx(
                out=basis_codes[:, g, :].bitcast(FP8X4),
                scales=basis_scales[:, g, :],
                in_=basis_bf[g][:].rearrange("p b u e -> p (b u e)"),
            )

        dist, wide_sq, narrow_sq, wide_cube, narrow_cube, uncut = [], [], [], [], [], []
        for g in range(PASSES):
            dist.append(work.tile([P, 2, P, 2], F32, name="dist"))
            wide_sq.append(work.tile([P, 2, P, 2], F32, name="wide_sq"))
            narrow_sq.append(work.tile([P, 2, P, 2], F32, name="narrow_sq"))
            wide_cube.append(work.tile([P, 2, P, 2], F32, name="wide_cube"))
            narrow_cube.append(work.tile([P, 2, P, 2], F32, name="narrow_cube"))
            uncut.append(work.tile([P, P, 2, 2], BF16, name="uncut"))
            basis_bf.append(work.tile([P, P, 2, 2], BF16, align_bytes=64, name="basis_g"))

        def flat(tile, es):
            return tile[:, es].rearrange("p e b u -> p (e b u)")

        def distance(g, e):
            nc.scalar.activation(
                out=dist[g][:, e], in_=u_ps[g][:].rearrange("p u b -> p b u"),
                func=ACT.Abs, scale=2.5, bias=centre[:, e : e + 1],
            )

        def square(out, root, centre_at, g, es):
            nc.scalar.activation(
                out=flat(out, es), in_=flat(dist[g], es), func=ACT.Square,
                scale=root, bias=-centre_at * root,
            )

        def cube(out, centre_at, g, es, sq):
            nc.vector.scalar_tensor_tensor(
                out=flat(out, es), in0=flat(dist[g], es),
                scalar=centre_at, in1=flat(sq, es), op0=ALU.subtract, op1=ALU.mult,
            )

        def combine(g):
            nc.vector.scalar_tensor_tensor(
                out=uncut[g][:].rearrange("p b u e -> p (b u) e"),
                in0=narrow_cube[g][:].rearrange("p e b u -> p (b u) e"),
                scalar=0.0, in1=wide_cube[g][:].rearrange("p e b u -> p (b u) e"),
                op0=ALU.min, op1=ALU.subtract,
            )

        def cut(g):
            nc.vector.tensor_scalar_max(
                out=basis_bf[g][:].rearrange("p b u e -> p (b u e)"),
                in0=uncut[g][:].rearrange("p b u e -> p (b u e)"), scalar1=0.0,
            )

        first, second, both = slice(0, 1), slice(1, 2), slice(0, 2)
        distance(0, 0)
        distance(0, 1)
        square(wide_sq[0], root_sixth, 2.0, 0, first)
        square(wide_sq[0], root_sixth, 2.0, 0, second)
        square(narrow_sq[0], root_two_thirds, 1.0, 0, both)
        distance(1, 0)
        distance(1, 1)
        square(wide_sq[1], root_sixth, 2.0, 1, first)
        square(wide_sq[1], root_sixth, 2.0, 1, second)
        square(narrow_sq[1], root_two_thirds, 1.0, 1, both)

        cube(wide_cube[0], 2.0, 0, first, wide_sq[0])
        cube(wide_cube[0], 2.0, 0, second, wide_sq[0])
        nc.vector.tensor_copy(out=rwT_sb[0][:], in_=rwT_ps[0])
        cube(narrow_cube[0], 1.0, 0, both, narrow_sq[0])
        nc.vector.tensor_copy(out=rwT_sb[1][:], in_=rwT_ps[1])
        combine(0)
        cube(wide_cube[1], 2.0, 1, both, wide_sq[1])
        cut(0)
        cube(narrow_cube[1], 1.0, 1, both, narrow_sq[1])
        quantise_basis(0)
        combine(1)
        nc.scalar.copy(out=bias_col[:], in_=small_ps[:, 1, 0:O_PAIRS].bitcast(BF16))

        out_ps = {}

        def open_pair(h):
            out_h = psum.tile([P, 2, P], F32, name="out_h", tag=OUT_BANKS[h])
            nc.tensor.matmul(
                out=out_h[:].rearrange("b t p -> b (t p)"),
                lhsT=xT_sb[:],
                rhs=rwT_sb[h // 2][:, 2 * (h % 2) : 2 * (h % 2) + 2, :].rearrange("i c p -> i (c p)"),
                start=True,
                stop=False,
            )
            out_ps[h] = out_h

        for c in range(6):
            transpose_tile(c)
        open_pair(0)
        open_pair(1)
        for c in range(O_TILES - 1):
            regroup(c)
            if c in (2, 3):
                transpose_tile(c + 4)
        for g in range(PASSES):
            regroup(O_TILES - 1, slice(g, g + 1))
        direct_ps = psum.tile([P, 4, P], F32, tag=OUT_BANKS[3])
        for n in range(2):
            c = PAIRED + n
            nc.tensor.transpose(
                direct_ps[:, 2 + n, :], base_sum[:, c : c + 1].to_broadcast([P, P]), ident_f32[:]
            )
        quantise_coef(0)
        cut(1)
        quantise_coef(1)
        quantise_basis(1)
        for c in range(2, O_TILES - 1):
            quantise_coef(c)
        for g in range(PASSES):
            quantise_coef(O_TILES - 1, slice(g, g + 1))

        spline_ps = {}
        scaled_sb = {}

        def multiply(tiles):
            spline = psum.tile([P, len(tiles), P], F32, name="spline", tag=SPLINE_BANKS[tiles[0]])
            for n, c in enumerate(tiles):
                for g in range(PASSES):
                    cols = slice(g * P, (g + 1) * P)
                    nc.tensor.matmul_mx(
                        out=spline[:, n, :],
                        lhsT=coef_codes[:, c, cols].bitcast(FP8X4),
                        lhsT_scale=coef_scales[:, c, cols],
                        rhs=basis_codes[:, g, :].bitcast(FP8X4),
                        rhs_scale=basis_scales[:, g, :],
                        start=(g == 0),
                        stop=(g == PASSES - 1),
                    )
                spline_ps[c] = spline[:, n, :]

        def multiply_direct():
            spline = psum.tile([P, 2, P], F32, name="spline_direct", tag=SPLINE_BANKS[PAIRED])
            for n in range(2):
                for g in range(PASSES):
                    cols = slice(g * P, (g + 1) * P)
                    nc.tensor.matmul_mx(
                        out=spline[:, n, :],
                        lhsT=basis_codes[:, g, :].bitcast(FP8X4),
                        lhsT_scale=basis_scales[:, g, :],
                        rhs=coef_codes[:, PAIRED + n, cols].bitcast(FP8X4),
                        rhs_scale=coef_scales[:, PAIRED + n, cols],
                        start=(g == 0),
                        stop=(g == PASSES - 1),
                    )
            return spline

        def scale_tile(c):
            scaled = stage.tile([P, P], F32, name="scaled")
            nc.scalar.activation(
                out=scaled[:], in_=spline_ps[c], func=ACT.Identity,
                scale=base_sum[:, c : c + 1], bias=bias_col[:, c : c + 1],
            )
            scaled_sb[c] = scaled

        def add_pair(h):
            for t in range(2):
                nc.tensor.matmul(
                    out=out_ps[h][:, t, :], lhsT=scaled_sb[2 * h + t][:], rhs=ident_f32[:],
                    is_transpose=True, start=False, stop=(t == 1),
                )

        def store_pair(h, copy):
            out_sb = stage.tile([P, P, 2], F32, name="out_sb")
            copy(out=out_sb[:], in_=out_ps[h][:].rearrange("b t p -> b p t"))
            nc.sync.dma_start(
                out=out[:, 2 * h * P : 2 * (h + 1) * P],
                in_=out_sb[:].rearrange("b p t -> b (p t)"),
            )

        multiply((0, 1))
        multiply((2, 3))
        open_pair(2)
        nc.tensor.matmul(
            out=direct_ps[:, 0:2, :], lhsT=xT_sb[:],
            rhs=rwT_sb[1][:, 2:4, :], start=True, stop=False,
        )
        nc.tensor.matmul(
            out=direct_ps[:, 0:2, :], lhsT=ident_bf[:, O_PAIRS - 1 : O_PAIRS].to_broadcast([P, P]),
            rhs=bias_rows[:].rearrange("k (p t) -> k t p", t=2), start=False, stop=True,
        )
        multiply((4, 5))
        for c in range(PAIRED):
            scale_tile(c)
        add_pair(0)
        direct_spline = multiply_direct()
        for h in range(1, PAIRED // 2):
            add_pair(h)
        scale_wide = stage.tile([P, 2, P], F32)
        nc.vector.tensor_copy(out=scale_wide[:], in_=direct_ps[:, 2:4, :])
        product = stage.tile([P, 2, P], F32)
        nc.vector.tensor_mul(out=product[:], in0=direct_spline[:], in1=scale_wide[:])
        store_pair(0, nc.scalar.copy)
        store_pair(1, nc.scalar.copy)
        direct_sb = stage.tile([P, P, 2], F32)
        nc.vector.tensor_add(
            out=direct_sb[:], in0=direct_ps[:, 0:2, :].rearrange("b t p -> b p t"),
            in1=product[:].rearrange("b t p -> b p t"),
        )
        store_pair(2, nc.scalar.copy)
        nc.sync.dma_start(out=out[:, PAIRED * P :], in_=direct_sb[:].rearrange("b p t -> b (p t)"))
